import numpy as np
import ml_dtypes


def mxq(x, axis, fmt="e4m3"):
    dtype, down = {"e4m3": (ml_dtypes.float8_e4m3fn, 7), "e5m2": (ml_dtypes.float8_e5m2, 14)}[fmt]
    v = np.moveaxis(np.asarray(x, np.float32).astype(ml_dtypes.bfloat16).astype(np.float64), axis, -1)
    blocks = v.reshape(v.shape[:-1] + (-1, 32))
    amax = np.abs(blocks).max(-1, keepdims=True)
    byte = np.maximum(np.where(amax > 0, np.frexp(amax)[1] - 1 + 127, 0) - down, 1)
    scale = np.exp2(byte - 127.0)
    codes = (blocks / scale).astype(np.float32).astype(dtype).astype(np.float64)
    return np.moveaxis((codes * scale).reshape(v.shape), -1, axis)


WIDE = False


def mx_kscale(k):
    if not WIDE:
        return np.ones(k)
    levels = np.array([10, -10, 5, -5, 0])
    a = np.random.permutation(np.resize(levels, k // 512 * 4)).reshape(k // 512, 4)
    idx = np.arange(k)
    return np.exp2(a[idx // 512, idx % 128 // 32])


BF16 = ml_dtypes.bfloat16


def bf(x):
    return np.asarray(x, np.float32).astype(BF16)


def f64(x):
    return np.asarray(x).astype(np.float64)


B, L, D, CH, S, R, NL = 1, 384, 1024, 2, 8, 128, 4
EPS = 1e-6


def rmsnorm(v, w):
    return v / np.sqrt(np.mean(v * v, axis=-1, keepdims=True) + EPS) * w


def setup_inputs():
    n = np.random.standard_normal
    t = mx_kscale(CH * D)
    tc = t.reshape(CH, D)[:, :, None]
    return {"x": bf(n((B, L, D))),
            "step_emb": bf(n(D) * 0.3),
            "w_in": bf(n((CH * D, D)) / np.sqrt(D)),
            "real": bf(n((B, L, CH, D, S)) * 1.2),
            "imag": bf(n((B, L, CH, D, S)) * 1.2),
            "A_theta": bf(n((CH, D, S)) * 0.5),
            "B_real": bf(n((CH, D, S)) * 0.5),
            "B_imag": bf(n((CH, D, S)) * 0.5),
            "C_real": bf(n((CH, D, S)) * 0.7 / np.sqrt(S) * tc),
            "C_imag": bf(n((CH, D, S)) * 0.7 / np.sqrt(S) * tc),
            "out_proj_w": bf(n((D, CH * D)) / np.sqrt(CH * D) / t[None, :]),
            "mixer_norm_w": bf(1.0 + 0.1 * n(D)),
            "loop_norm_w": bf(1.0 + 0.1 * n(D))}


def reference(x, step_emb, w_in, real, imag, A_theta, B_real, B_imag, C_real, C_imag, out_proj_w, mixer_norm_w, loop_norm_w):
    h = f64(x) + f64(step_emb)
    x_in = (mxq(h, 2, "e4m3") @ mxq(f64(w_in), 1, "e4m3").T).reshape(B, L, CH, D)[..., None]
    cos_t = np.cos(f64(A_theta))[None, None]
    sin_t = np.sin(f64(A_theta))[None, None]
    Br = f64(B_real)[None, None]
    Bi = f64(B_imag)[None, None]
    Cr = f64(C_real)[None, None]
    Ci = f64(C_imag)[None, None]
    re = f64(real)
    im = f64(imag)
    new_real = cos_t * re - sin_t * im + Br * x_in
    new_imag = sin_t * re + cos_t * im + Bi * x_in
    y = (Cr * new_real - Ci * new_imag).sum(-1).reshape(B, L, CH * D)
    out = rmsnorm(mxq(y, 2, "e4m3") @ mxq(f64(out_proj_w), 1, "e4m3").T, f64(mixer_norm_w))
    return rmsnorm(h + out, f64(loop_norm_w))

@@ -1,0 +1,368 @@
+from contextlib import ExitStack
+import math
+
+import concourse.mybir as mybir
+from concourse.masks import make_identity
+
+F32 = mybir.dt.float32
+BF16 = mybir.dt.bfloat16
+U32 = mybir.dt.uint32
+U8 = mybir.dt.uint8
+FP8X4 = mybir.dt.float8_e4m3fn_x4
+ALU = mybir.AluOpType
+ACT = mybir.ActivationFunctionType
+AXIS = mybir.AxisListType
+
+P = 128
+L = 384
+D = 1024
+F = 2048
+S = 8
+EPS = 1e-6
+
+L_TILES = L // P
+K_PASS = 512
+PAIRS = F // 256
+TILES = 2 * PAIRS
+WORDS = S // 2
+BANK = 512
+
+ROUND_MAGIC = 12582912.0
+TWO_PI_HIGH = 6.28125
+TWO_PI_LOW = 2.0 * math.pi - TWO_PI_HIGH
+PI_BELOW = 3.1415925
+
+FLOPS = 2 * L * D * F + 2 * L * F * D + 2 * 2 * S * L * F
+
+
+def tile_recursivemamba130m_pa_kernel(
+    tc,
+    x,
+    step_emb,
+    w_in,
+    real,
+    imag,
+    A_theta,
+    B_real,
+    B_imag,
+    C_real,
+    C_imag,
+    out_proj_w,
+    mixer_norm_w,
+    loop_norm_w,
+    out,
+):
+    nc = tc.nc
+    with ExitStack() as ctx:
+        keep = ctx.enter_context(tc.tile_pool(name="keep", bufs=1))
+        stream = ctx.enter_context(tc.tile_pool(name="stream", bufs=12))
+        weights = ctx.enter_context(tc.tile_pool(name="weights", bufs=2))
+        stage = ctx.enter_context(tc.tile_pool(name="stage", bufs=3))
+        sums = ctx.enter_context(tc.tile_pool(name="sums", bufs=2))
+        tail = ctx.enter_context(tc.tile_pool(name="tail", bufs=2))
+        psum = ctx.enter_context(tc.psum_pool(name="psum", bufs=8))
+
+        ident_f32 = keep.tile([P, P], F32, name="ident_f32")
+        make_identity(nc, ident_f32[:])
+        ident_bf16 = keep.tile([P, P], BF16, name="ident_bf16")
+        make_identity(nc, ident_bf16[:])
+
+        state_rows = {
+            "real": real.rearrange("b l c d s -> (b l) (c d s)"),
+            "imag": imag.rearrange("b l c d s -> (b l) (c d s)"),
+        }
+        w_in_pairs = w_in.rearrange("(q p e) k -> q p e k", p=P, e=2)
+        w_out_blocks = out_proj_w.rearrange("(r i p) k -> r p i k", i=2, p=P)
+
+        def load_table(table, name):
+            raw = keep.tile([P, PAIRS, 2 * S], BF16, name=name)
+            nc.sync.dma_start(
+                out=raw[:],
+                in_=table.rearrange("c d s -> (c d) s").rearrange(
+                    "(q p e) s -> p q (e s)", p=P, e=2
+                ),
+            )
+            return raw[:].rearrange("p q f -> p (q f)")
+
+        def load_pair(q):
+            w_raw = weights.tile([P, 2, D], BF16, tag="w_raw")
+            nc.sync.dma_start(out=w_raw[:], in_=w_in_pairs[q])
+            chunks = {}
+            for which in ("real", "imag"):
+                for t in range(L_TILES):
+                    chunk = stream.tile([P, 256 * S], BF16, tag="chunk")
+                    nc.sync.dma_start(
+                        out=chunk[:],
+                        in_=state_rows[which][t * P : (t + 1) * P, q * 256 * S : (q + 1) * 256 * S],
+                    )
+                    chunks[(which, t)] = chunk
+            return w_raw, chunks
+
+        x_sb = keep.tile([P, L_TILES, D], BF16, name="x_sb")
+        nc.sync.dma_start(out=x_sb[:], in_=x.rearrange("b (t p) d -> p (b t) d", p=P))
+        emb_rows = keep.tile([P, D], BF16, name="emb_rows")
+        nc.sync.dma_start(out=emb_rows[:], in_=step_emb.partition_broadcast(P))
+        theta = load_table(A_theta, "theta")
+        c_re = load_table(C_real, "c_re")
+        c_im = load_table(C_imag, "c_im")
+        b_re = load_table(B_real, "b_re")
+        b_im = load_table(B_imag, "b_im")
+        loaded = load_pair(0)
+
+        h_codes = keep.tile([P, D // K_PASS, L], U32, name="h_codes", align_bytes=64)
+        h_scales = keep.tile([P, D // K_PASS, L], U8, name="h_scales", align_bytes=64)
+        w1_codes = keep.tile([P, D // K_PASS, F], U32, name="w1_codes", align_bytes=64)
+        w1_scales = keep.tile([P, D // K_PASS, F], U8, name="w1_scales", align_bytes=64)
+        y_codes = keep.tile([P, F // K_PASS, L], U32, name="y_codes", align_bytes=64)
+        y_scales = keep.tile([P, F // K_PASS, L], U8, name="y_scales", align_bytes=64)
+        w2_codes = keep.tile([P, F // K_PASS, D], U32, name="w2_codes", align_bytes=64)
+        w2_scales = keep.tile([P, F // K_PASS, D], U8, name="w2_scales", align_bytes=64)
+
+        def quantise_weight_rows(raw, passes, codes, scales, col0):
+            raw_words = raw.bitcast(F32)
+            for g in range(passes):
+                turned = psum.tile([P, BANK], F32, tag="bank")
+                for u in range(2):
+                    for i in range(2):
+                        first = 256 * g + 128 * u
+                        nc.tensor.transpose(
+                            turned[:, (2 * u + i) * P : (2 * u + i + 1) * P],
+                            raw_words[:, i, first : first + P],
+                            ident_f32[:],
+                        )
+                grouped = stage.tile([P, 4 * 256], BF16, tag="grouped_w", align_bytes=64)
+                nc.scalar.copy(
+                    out=grouped[:].bitcast(F32).rearrange("p (r u) -> p r u", u=2),
+                    in_=turned[:].rearrange("p (u r) -> p r u", u=2),
+                )
+                nc.vector.quantize_mx(
+                    out=codes[:, g, col0 : col0 + 256].bitcast(FP8X4),
+                    scales=scales[:, g, col0 : col0 + 256],
+                    in_=grouped[:],
+                )
+
+        h_bf16 = keep.tile([P, L_TILES, D], BF16, name="h_bf16")
+        for t in range(L_TILES):
+            nc.vector.tensor_tensor(
+                out=h_bf16[:, t, :], in0=x_sb[:, t, :], in1=emb_rows[:], op=ALU.add
+            )
+            columns = h_bf16[:, t, :].rearrange("l (g u p e) -> l g u p e", g=2, u=2, e=2)
+            turned_h = psum.tile([P, 2 * BANK], BF16, tag="bank")
+            for g in range(2):
+                for u in range(2):
+                    for e in range(2):
+                        slot = 4 * g + 2 * u + e
+                        nc.tensor.transpose(
+                            turned_h[:, slot * P : (slot + 1) * P],
+                            columns[:, g, u, :, e],
+                            ident_bf16[:],
+                        )
+            grouped_h = stage.tile([P, 2, P, 4], BF16, tag="grouped_h", align_bytes=64)
+            nc.scalar.copy(
+                out=grouped_h[:], in_=turned_h[:].rearrange("p (g k l) -> p g l k", g=2, k=4)
+            )
+            for g in range(2):
+                nc.vector.quantize_mx(
+                    out=h_codes[:, g, t * P : (t + 1) * P].bitcast(FP8X4),
+                    scales=h_scales[:, g, t * P : (t + 1) * P],
+                    in_=grouped_h[:, g].rearrange("p l k -> p (l k)"),
+                )
+
+        h_f32 = keep.tile([P, L_TILES, D], F32, name="h_f32")
+        for t in range(L_TILES):
+            nc.gpsimd.tensor_tensor(
+                out=h_f32[:, t, :], in0=x_sb[:, t, :], in1=emb_rows[:], op=ALU.add
+            )
+
+        def table(name):
+            return keep.tile([P, TILES * S], F32, name=name)
+
+        turns = table("turns")
+        nc.vector.tensor_scalar(
+            out=turns[:], in0=theta, scalar1=1.0 / (2.0 * math.pi), scalar2=ROUND_MAGIC,
+            op0=ALU.mult, op1=ALU.add,
+        )
+        nc.vector.tensor_scalar_sub(out=turns[:], in0=turns[:], scalar1=ROUND_MAGIC)
+        angle = table("angle")
+        nc.vector.scalar_tensor_tensor(
+            out=angle[:], in0=turns[:], scalar=-TWO_PI_HIGH, in1=theta, op0=ALU.mult, op1=ALU.add
+        )
+        nc.vector.scalar_tensor_tensor(
+            out=angle[:], in0=turns[:], scalar=-TWO_PI_LOW, in1=angle[:], op0=ALU.mult, op1=ALU.add
+        )
+        nc.vector.tensor_scalar(
+            out=angle[:], in0=angle[:], scalar1=-PI_BELOW, scalar2=PI_BELOW, op0=ALU.max, op1=ALU.min
+        )
+        sin_t = table("sin_t")
+        nc.scalar.activation(out=sin_t[:], in_=angle[:], func=ACT.Sin)
+        cos_t = table("cos_t")
+        nc.scalar.activation(out=cos_t[:], in_=angle[:], func=ACT.Sin, scale=0.5)
+        nc.vector.tensor_tensor(out=cos_t[:], in0=cos_t[:], in1=cos_t[:], op=ALU.mult)
+        nc.vector.tensor_scalar(
+            out=cos_t[:], in0=cos_t[:], scalar1=-2.0, scalar2=1.0, op0=ALU.mult, op1=ALU.add
+        )
+
+        def product(name, a, b):
+            result = table(name)
+            nc.vector.tensor_tensor(out=result[:], in0=a, in1=b, op=ALU.mult)
+            return result
+
+        coef = {"real": table("coef_real"), "imag": table("coef_imag")}
+        re_cos = product("re_cos", c_re, cos_t[:])
+        im_sin = product("im_sin", c_im, sin_t[:])
+        nc.vector.tensor_tensor(out=coef["real"][:], in0=re_cos[:], in1=im_sin[:], op=ALU.subtract)
+        re_sin = product("re_sin", c_re, sin_t[:])
+        im_cos = product("im_cos", c_im, cos_t[:])
+        nc.vector.scalar_tensor_tensor(
+            out=coef["imag"][:], in0=re_sin[:], scalar=-1.0, in1=im_cos[:],
+            op0=ALU.mult, op1=ALU.subtract,
+        )
+        re_re = product("re_re", c_re, b_re)
+        im_im = product("im_im", c_im, b_im)
+        nc.vector.tensor_tensor(out=re_re[:], in0=re_re[:], in1=im_im[:], op=ALU.subtract)
+        gain = keep.tile([P, TILES], F32, name="gain")
+        nc.vector.tensor_reduce(
+            out=gain[:], in_=re_re[:].rearrange("p (c s) -> p c s", s=S), axis=AXIS.X, op=ALU.add
+        )
+
+        y_sum = None
+        for q in range(PAIRS):
+            g, u = divmod(q, 2)
+            w_raw, chunks = loaded
+            if q + 1 < PAIRS:
+                loaded = load_pair(q + 1)
+            if u == 1:
+                w_out_raw = weights.tile([P, 2, F], BF16, tag="w_out_raw")
+                nc.sync.dma_start(out=w_out_raw[:], in_=w_out_blocks[g])
+
+            quantise_weight_rows(w_raw[:], D // K_PASS, w1_codes, w1_scales, 256 * q)
+
+            if u == 0:
+                y_sum = sums.tile([P, 4, L], F32, tag="y_sum")
+
+            for e in range(2):
+                x_in = psum.tile([P, BANK], F32, tag="bank")
+                cols = slice(256 * q + P * e, 256 * q + P * (e + 1))
+                for n0, n in ((0, 256), (256, 128)):
+                    for c in range(D // K_PASS):
+                        nc.tensor.matmul_mx(
+                            out=x_in[:, n0 : n0 + n],
+                            lhsT=w1_codes[:, c, cols].bitcast(FP8X4),
+                            lhsT_scale=w1_scales[:, c, cols],
+                            rhs=h_codes[:, c, n0 : n0 + n].bitcast(FP8X4),
+                            rhs_scale=h_scales[:, c, n0 : n0 + n],
+                            start=(c == 0),
+                            stop=(c == D // K_PASS - 1),
+                        )
+                nc.scalar.activation(
+                    out=y_sum[:, 2 * u + e, :], in_=x_in[:, 0:L], func=ACT.Copy,
+                    scale=gain[:, 2 * q + e : 2 * q + e + 1],
+                )
+
+            for which in ("real", "imag"):
+                for w in range(WORDS):
+                    turned = []
+                    for e in range(2):
+                        bank = psum.tile([P, BANK], F32, tag="bank")
+                        for t in range(L_TILES):
+                            words = chunks[(which, t)][:].bitcast(F32).rearrange(
+                                "l (p j) -> l p j", j=2 * WORDS
+                            )
+                            nc.tensor.transpose(
+                                bank[:, t * P : (t + 1) * P], words[:, :, WORDS * e + w], ident_f32[:]
+                            )
+                        turned.append(bank[:].bitcast(BF16).rearrange("p (l h) -> p l h", h=2))
+                    for h in range(2):
+                        for e in range(2):
+                            column = (2 * q + e) * S + 2 * w + h
+                            nc.vector.scalar_tensor_tensor(
+                                out=y_sum[:, 2 * u + e, :],
+                                in0=turned[e][:, 0:L, h],
+                                scalar=coef[which][:, column : column + 1],
+                                in1=y_sum[:, 2 * u + e, :],
+                                op0=ALU.mult,
+                                op1=ALU.add,
+                            )
+
+            if u == 1:
+                quantise_weight_rows(w_out_raw[:], F // K_PASS, w2_codes, w2_scales, 256 * g)
+                for t in range(L_TILES):
+                    grouped_y = stage.tile([P, P, 4], BF16, tag="grouped_y", align_bytes=64)
+                    nc.scalar.copy(
+                        out=grouped_y[:],
+                        in_=y_sum[:, :, t * P : (t + 1) * P].rearrange("p k l -> p l k"),
+                    )
+                    nc.vector.quantize_mx(
+                        out=y_codes[:, g, t * P : (t + 1) * P].bitcast(FP8X4),
+                        scales=y_scales[:, g, t * P : (t + 1) * P],
+                        in_=grouped_y[:].rearrange("p l k -> p (l k)"),
+                    )
+
+        mixer_rows = keep.tile([P, D], BF16, name="mixer_rows")
+        nc.sync.dma_start(out=mixer_rows[:], in_=mixer_norm_w.partition_broadcast(P))
+        loop_rows = keep.tile([P, D], BF16, name="loop_rows")
+        nc.sync.dma_start(out=loop_rows[:], in_=loop_norm_w.partition_broadcast(P))
+        out_tiles = out.rearrange("b (t p) d -> (b t) p d", p=P)
+        HALVES = D // BANK
+
+        def inverse_rms(square_sums):
+            mean = tail.tile([P, 1], F32, tag="mean")
+            nc.vector.tensor_tensor(
+                out=mean[:], in0=square_sums[:, 0:1], in1=square_sums[:, 1:2], op=ALU.add
+            )
+            nc.vector.tensor_scalar(
+                out=mean[:], in0=mean[:], scalar1=1.0 / D, scalar2=EPS, op0=ALU.mult, op1=ALU.add
+            )
+            nc.scalar.sqrt(out=mean[:], in_=mean[:])
+            inverse = tail.tile([P, 1], F32, tag="inverse")
+            nc.vector.reciprocal(out=inverse[:], in_=mean[:])
+            return inverse
+
+        for t in range(L_TILES):
+            rows = slice(t * P, (t + 1) * P)
+            projected = []
+            proj_squares = tail.tile([P, HALVES], F32, tag="proj_squares")
+            for half in range(HALVES):
+                proj = psum.tile([P, BANK], F32, tag="bank")
+                for g in range(F // K_PASS):
+                    nc.tensor.matmul_mx(
+                        out=proj[:],
+                        lhsT=y_codes[:, g, rows].bitcast(FP8X4),
+                        lhsT_scale=y_scales[:, g, rows],
+                        rhs=w2_codes[:, g, half * BANK : (half + 1) * BANK].bitcast(FP8X4),
+                        rhs_scale=w2_scales[:, g, half * BANK : (half + 1) * BANK],
+                        start=(g == 0),
+                        stop=(g == F // K_PASS - 1),
+                    )
+                squared = tail.tile([P, BANK], F32, tag="squared")
+                nc.scalar.activation(
+                    out=squared[:], in_=proj[:], func=ACT.Square,
+                    accum_out=proj_squares[:, half : half + 1],
+                )
+                projected.append(proj)
+            proj_scale = inverse_rms(proj_squares)
+
+            residual = tail.tile([P, D], F32, tag="residual")
+            res_squares = tail.tile([P, HALVES], F32, tag="res_squares")
+            for half in range(HALVES):
+                cols = slice(half * BANK, (half + 1) * BANK)
+                nc.vector.scalar_tensor_tensor(
+                    out=residual[:, cols], in0=projected[half][:], scalar=proj_scale[:, 0:1],
+                    in1=mixer_rows[:, cols], op0=ALU.mult, op1=ALU.mult,
+                )
+                nc.vector.tensor_tensor(
+                    out=residual[:, cols], in0=residual[:, cols], in1=h_f32[:, t, cols], op=ALU.add
+                )
+                squared = tail.tile([P, BANK], F32, tag="squared")
+                nc.scalar.activation(
+                    out=squared[:], in_=residual[:, cols], func=ACT.Square,
+                    accum_out=res_squares[:, half : half + 1],
+                )
+            res_scale = inverse_rms(res_squares)
+
+            result = tail.tile([P, D], F32, tag="result")
+            nc.vector.scalar_tensor_tensor(
+                out=result[:], in0=residual[:], scalar=res_scale[:, 0:1], in1=loop_rows[:],
+                op0=ALU.mult, op1=ALU.mult,
+            )
+            nc.sync.dma_start(out=out_tiles[t], in_=result[:])

@@ -26,6 +26,7 @@ PAIRS = F // 256
 TILES = 2 * PAIRS
 WORDS = S // 2
 BANK = 512
+SLOW_WORDS = 2
 
 ROUND_MAGIC = 12582912.0
 TWO_PI_HIGH = 6.28125
@@ -53,61 +54,15 @@ def tile_recursivemamba130m_pa_kernel(
     out,
 ):
     nc = tc.nc
-    with ExitStack() as ctx:
-        keep = ctx.enter_context(tc.tile_pool(name="keep", bufs=1))
-        stream = ctx.enter_context(tc.tile_pool(name="stream", bufs=12))
-        weights = ctx.enter_context(tc.tile_pool(name="weights", bufs=2))
-        stage = ctx.enter_context(tc.tile_pool(name="stage", bufs=3))
-        sums = ctx.enter_context(tc.tile_pool(name="sums", bufs=2))
-        tail = ctx.enter_context(tc.tile_pool(name="tail", bufs=2))
-        psum = ctx.enter_context(tc.psum_pool(name="psum", bufs=8))
+    with ExitStack() as whole:
+        keep = whole.enter_context(tc.tile_pool(name="keep", bufs=1))
 
         ident_f32 = keep.tile([P, P], F32, name="ident_f32")
         make_identity(nc, ident_f32[:])
         ident_bf16 = keep.tile([P, P], BF16, name="ident_bf16")
         make_identity(nc, ident_bf16[:])
-
-        state_rows = {
-            "real": real.rearrange("b l c d s -> (b l) (c d s)"),
-            "imag": imag.rearrange("b l c d s -> (b l) (c d s)"),
-        }
-        w_in_pairs = w_in.rearrange("(q p e) k -> q p e k", p=P, e=2)
-        w_out_blocks = out_proj_w.rearrange("(r i p) k -> r p i k", i=2, p=P)
-
-        def load_table(table, name):
-            raw = keep.tile([P, PAIRS, 2 * S], BF16, name=name)
-            nc.sync.dma_start(
-                out=raw[:],
-                in_=table.rearrange("c d s -> (c d) s").rearrange(
-                    "(q p e) s -> p q (e s)", p=P, e=2
-                ),
-            )
-            return raw[:].rearrange("p q f -> p (q f)")
-
-        def load_pair(q):
-            w_raw = weights.tile([P, 2, D], BF16, tag="w_raw")
-            nc.sync.dma_start(out=w_raw[:], in_=w_in_pairs[q])
-            chunks = {}
-            for which in ("real", "imag"):
-                for t in range(L_TILES):
-                    chunk = stream.tile([P, 256 * S], BF16, tag="chunk")
-                    nc.sync.dma_start(
-                        out=chunk[:],
-                        in_=state_rows[which][t * P : (t + 1) * P, q * 256 * S : (q + 1) * 256 * S],
-                    )
-                    chunks[(which, t)] = chunk
-            return w_raw, chunks
-
-        x_sb = keep.tile([P, L_TILES, D], BF16, name="x_sb")
-        nc.sync.dma_start(out=x_sb[:], in_=x.rearrange("b (t p) d -> p (b t) d", p=P))
-        emb_rows = keep.tile([P, D], BF16, name="emb_rows")
-        nc.sync.dma_start(out=emb_rows[:], in_=step_emb.partition_broadcast(P))
-        theta = load_table(A_theta, "theta")
-        c_re = load_table(C_real, "c_re")
-        c_im = load_table(C_imag, "c_im")
-        b_re = load_table(B_real, "b_re")
-        b_im = load_table(B_imag, "b_im")
-        loaded = load_pair(0)
+        eps_column = keep.tile([P, 1], F32, name="eps_column")
+        nc.vector.memset(eps_column[:], EPS)
 
         h_codes = keep.tile([P, D // K_PASS, L], U32, name="h_codes", align_bytes=64)
         h_scales = keep.tile([P, D // K_PASS, L], U8, name="h_scales", align_bytes=64)
@@ -117,252 +72,355 @@ def tile_recursivemamba130m_pa_kernel(
         y_scales = keep.tile([P, F // K_PASS, L], U8, name="y_scales", align_bytes=64)
         w2_codes = keep.tile([P, F // K_PASS, D], U32, name="w2_codes", align_bytes=64)
         w2_scales = keep.tile([P, F // K_PASS, D], U8, name="w2_scales", align_bytes=64)
-
-        def quantise_weight_rows(raw, passes, codes, scales, col0):
-            raw_words = raw.bitcast(F32)
-            for g in range(passes):
-                turned = psum.tile([P, BANK], F32, tag="bank")
-                for u in range(2):
-                    for i in range(2):
-                        first = 256 * g + 128 * u
-                        nc.tensor.transpose(
-                            turned[:, (2 * u + i) * P : (2 * u + i + 1) * P],
-                            raw_words[:, i, first : first + P],
-                            ident_f32[:],
-                        )
-                grouped = stage.tile([P, 4 * 256], BF16, tag="grouped_w", align_bytes=64)
-                nc.scalar.copy(
-                    out=grouped[:].bitcast(F32).rearrange("p (r u) -> p r u", u=2),
-                    in_=turned[:].rearrange("p (u r) -> p r u", u=2),
-                )
-                nc.vector.quantize_mx(
-                    out=codes[:, g, col0 : col0 + 256].bitcast(FP8X4),
-                    scales=scales[:, g, col0 : col0 + 256],
-                    in_=grouped[:],
-                )
-
-        h_bf16 = keep.tile([P, L_TILES, D], BF16, name="h_bf16")
-        for t in range(L_TILES):
-            nc.vector.tensor_tensor(
-                out=h_bf16[:, t, :], in0=x_sb[:, t, :], in1=emb_rows[:], op=ALU.add
-            )
-            columns = h_bf16[:, t, :].rearrange("l (g u p e) -> l g u p e", g=2, u=2, e=2)
-            turned_h = psum.tile([P, 2 * BANK], BF16, tag="bank")
-            for g in range(2):
-                for u in range(2):
-                    for e in range(2):
-                        slot = 4 * g + 2 * u + e
-                        nc.tensor.transpose(
-                            turned_h[:, slot * P : (slot + 1) * P],
-                            columns[:, g, u, :, e],
-                            ident_bf16[:],
-                        )
-            grouped_h = stage.tile([P, 2, P, 4], BF16, tag="grouped_h", align_bytes=64)
-            nc.scalar.copy(
-                out=grouped_h[:], in_=turned_h[:].rearrange("p (g k l) -> p g l k", g=2, k=4)
-            )
-            for g in range(2):
-                nc.vector.quantize_mx(
-                    out=h_codes[:, g, t * P : (t + 1) * P].bitcast(FP8X4),
-                    scales=h_scales[:, g, t * P : (t + 1) * P],
-                    in_=grouped_h[:, g].rearrange("p l k -> p (l k)"),
-                )
-
         h_f32 = keep.tile([P, L_TILES, D], F32, name="h_f32")
-        for t in range(L_TILES):
-            nc.gpsimd.tensor_tensor(
-                out=h_f32[:, t, :], in0=x_sb[:, t, :], in1=emb_rows[:], op=ALU.add
-            )
+        mixer_rows = keep.tile([P, D], BF16, name="mixer_rows")
+        loop_rows = keep.tile([P, D], BF16, name="loop_rows")
 
-        def table(name):
-            return keep.tile([P, TILES * S], F32, name=name)
+        with ExitStack() as body:
+            stream = body.enter_context(tc.tile_pool(name="stream", bufs=18))
+            weights = body.enter_context(tc.tile_pool(name="weights", bufs=2))
+            stage = body.enter_context(tc.tile_pool(name="stage", bufs=3))
+            sums = body.enter_context(tc.tile_pool(name="sums", bufs=2))
+            products = body.enter_context(tc.tile_pool(name="products", bufs=4))
+            psum = body.enter_context(tc.psum_pool(name="psum", bufs=4))
 
-        turns = table("turns")
-        nc.vector.tensor_scalar(
-            out=turns[:], in0=theta, scalar1=1.0 / (2.0 * math.pi), scalar2=ROUND_MAGIC,
-            op0=ALU.mult, op1=ALU.add,
-        )
-        nc.vector.tensor_scalar_sub(out=turns[:], in0=turns[:], scalar1=ROUND_MAGIC)
-        angle = table("angle")
-        nc.vector.scalar_tensor_tensor(
-            out=angle[:], in0=turns[:], scalar=-TWO_PI_HIGH, in1=theta, op0=ALU.mult, op1=ALU.add
-        )
-        nc.vector.scalar_tensor_tensor(
-            out=angle[:], in0=turns[:], scalar=-TWO_PI_LOW, in1=angle[:], op0=ALU.mult, op1=ALU.add
-        )
-        nc.vector.tensor_scalar(
-            out=angle[:], in0=angle[:], scalar1=-PI_BELOW, scalar2=PI_BELOW, op0=ALU.max, op1=ALU.min
-        )
-        sin_t = table("sin_t")
-        nc.scalar.activation(out=sin_t[:], in_=angle[:], func=ACT.Sin)
-        cos_t = table("cos_t")
-        nc.scalar.activation(out=cos_t[:], in_=angle[:], func=ACT.Sin, scale=0.5)
-        nc.vector.tensor_tensor(out=cos_t[:], in0=cos_t[:], in1=cos_t[:], op=ALU.mult)
-        nc.vector.tensor_scalar(
-            out=cos_t[:], in0=cos_t[:], scalar1=-2.0, scalar2=1.0, op0=ALU.mult, op1=ALU.add
-        )
+            state_rows = {
+                "real": real.rearrange("b l c d s -> (b l) (c d s)"),
+                "imag": imag.rearrange("b l c d s -> (b l) (c d s)"),
+            }
+            w_in_pairs = w_in.rearrange("(q p e) k -> q p e k", p=P, e=2)
+            w_out_blocks = out_proj_w.rearrange("(r i p) k -> r p i k", i=2, p=P)
 
-        def product(name, a, b):
-            result = table(name)
-            nc.vector.tensor_tensor(out=result[:], in0=a, in1=b, op=ALU.mult)
-            return result
+            def load_table(table, name):
+                raw = keep.tile([P, PAIRS, 2 * S], BF16, name=name)
+                nc.sync.dma_start(
+                    out=raw[:],
+                    in_=table.rearrange("c d s -> (c d) s").rearrange(
+                        "(q p e) s -> p q (e s)", p=P, e=2
+                    ),
+                )
+                return raw[:].rearrange("p q f -> p (q f)")
 
-        coef = {"real": table("coef_real"), "imag": table("coef_imag")}
-        re_cos = product("re_cos", c_re, cos_t[:])
-        im_sin = product("im_sin", c_im, sin_t[:])
-        nc.vector.tensor_tensor(out=coef["real"][:], in0=re_cos[:], in1=im_sin[:], op=ALU.subtract)
-        re_sin = product("re_sin", c_re, sin_t[:])
-        im_cos = product("im_cos", c_im, cos_t[:])
-        nc.vector.scalar_tensor_tensor(
-            out=coef["imag"][:], in0=re_sin[:], scalar=-1.0, in1=im_cos[:],
-            op0=ALU.mult, op1=ALU.subtract,
-        )
-        re_re = product("re_re", c_re, b_re)
-        im_im = product("im_im", c_im, b_im)
-        nc.vector.tensor_tensor(out=re_re[:], in0=re_re[:], in1=im_im[:], op=ALU.subtract)
-        gain = keep.tile([P, TILES], F32, name="gain")
-        nc.vector.tensor_reduce(
-            out=gain[:], in_=re_re[:].rearrange("p (c s) -> p c s", s=S), axis=AXIS.X, op=ALU.add
-        )
-
-        y_sum = None
-        for q in range(PAIRS):
-            g, u = divmod(q, 2)
-            w_raw, chunks = loaded
-            if q + 1 < PAIRS:
-                loaded = load_pair(q + 1)
-            if u == 1:
-                w_out_raw = weights.tile([P, 2, F], BF16, tag="w_out_raw")
-                nc.sync.dma_start(out=w_out_raw[:], in_=w_out_blocks[g])
-
-            quantise_weight_rows(w_raw[:], D // K_PASS, w1_codes, w1_scales, 256 * q)
-
-            if u == 0:
-                y_sum = sums.tile([P, 4, L], F32, tag="y_sum")
-
-            for e in range(2):
-                x_in = psum.tile([P, BANK], F32, tag="bank")
-                cols = slice(256 * q + P * e, 256 * q + P * (e + 1))
-                for n0, n in ((0, 256), (256, 128)):
-                    for c in range(D // K_PASS):
-                        nc.tensor.matmul_mx(
-                            out=x_in[:, n0 : n0 + n],
-                            lhsT=w1_codes[:, c, cols].bitcast(FP8X4),
-                            lhsT_scale=w1_scales[:, c, cols],
-                            rhs=h_codes[:, c, n0 : n0 + n].bitcast(FP8X4),
-                            rhs_scale=h_scales[:, c, n0 : n0 + n],
-                            start=(c == 0),
-                            stop=(c == D // K_PASS - 1),
+            def load_pair(q):
+                w_raw = weights.tile([P, 2, D], BF16, tag="w_raw")
+                nc.sync.dma_start(out=w_raw[:], in_=w_in_pairs[q])
+                chunks = {}
+                for which in ("real", "imag"):
+                    for t in range(L_TILES):
+                        chunk = stream.tile([P, 256 * S], BF16, tag="chunk")
+                        nc.sync.dma_start(
+                            out=chunk[:],
+                            in_=state_rows[which][
+                                t * P : (t + 1) * P, q * 256 * S : (q + 1) * 256 * S
+                            ],
                         )
-                nc.scalar.activation(
-                    out=y_sum[:, 2 * u + e, :], in_=x_in[:, 0:L], func=ACT.Copy,
-                    scale=gain[:, 2 * q + e : 2 * q + e + 1],
+                        chunks[(which, t)] = chunk
+                return w_raw, chunks
+
+            x_sb = keep.tile([P, L_TILES, D], BF16, name="x_sb")
+            nc.sync.dma_start(out=x_sb[:], in_=x.rearrange("b (t p) d -> p (b t) d", p=P))
+            emb_rows = keep.tile([P, D], BF16, name="emb_rows")
+            nc.sync.dma_start(out=emb_rows[:], in_=step_emb.partition_broadcast(P))
+            theta = load_table(A_theta, "theta")
+            c_re = load_table(C_real, "c_re")
+            c_im = load_table(C_imag, "c_im")
+            b_re = load_table(B_real, "b_re")
+            b_im = load_table(B_imag, "b_im")
+            loaded = {0: load_pair(0), 1: load_pair(1)}
+
+            def quantise_weight_rows(raw, passes, codes, scales, col0):
+                raw_words = raw.bitcast(F32)
+                for g in range(passes):
+                    turned = psum.tile([P, BANK], F32, tag="for_scalar")
+                    for u in range(2):
+                        for i in range(2):
+                            first = 256 * g + 128 * u
+                            nc.tensor.transpose(
+                                turned[:, (2 * u + i) * P : (2 * u + i + 1) * P],
+                                raw_words[:, i, first : first + P],
+                                ident_f32[:],
+                            )
+                    grouped = stage.tile([P, 4 * 256], BF16, tag="grouped_w", align_bytes=64)
+                    nc.scalar.copy(
+                        out=grouped[:].bitcast(F32).rearrange("p (r u) -> p r u", u=2),
+                        in_=turned[:].rearrange("p (u r) -> p r u", u=2),
+                    )
+                    nc.vector.quantize_mx(
+                        out=codes[:, g, col0 : col0 + 256].bitcast(FP8X4),
+                        scales=scales[:, g, col0 : col0 + 256],
+                        in_=grouped[:],
+                    )
+
+            h_bf16 = keep.tile([P, L_TILES, D], BF16, name="h_bf16")
+            for t in range(L_TILES):
+                nc.vector.tensor_tensor(
+                    out=h_bf16[:, t, :], in0=x_sb[:, t, :], in1=emb_rows[:], op=ALU.add
+                )
+                columns = h_bf16[:, t, :].rearrange("l (g u p e) -> l g u p e", g=2, u=2, e=2)
+                turned_h = psum.tile([P, 2 * BANK], BF16, tag="for_scalar")
+                for g in range(2):
+                    for u in range(2):
+                        for e in range(2):
+                            slot = 4 * g + 2 * u + e
+                            nc.tensor.transpose(
+                                turned_h[:, slot * P : (slot + 1) * P],
+                                columns[:, g, u, :, e],
+                                ident_bf16[:],
+                            )
+                grouped_h = stage.tile([P, 2, P, 4], BF16, tag="grouped_h", align_bytes=64)
+                nc.scalar.copy(
+                    out=grouped_h[:], in_=turned_h[:].rearrange("p (g k l) -> p g l k", g=2, k=4)
+                )
+                for g in range(2):
+                    nc.vector.quantize_mx(
+                        out=h_codes[:, g, t * P : (t + 1) * P].bitcast(FP8X4),
+                        scales=h_scales[:, g, t * P : (t + 1) * P],
+                        in_=grouped_h[:, g].rearrange("p l k -> p (l k)"),
+                    )
+
+            for t in range(L_TILES):
+                nc.gpsimd.tensor_tensor(
+                    out=h_f32[:, t, :], in0=x_sb[:, t, :], in1=emb_rows[:], op=ALU.add
                 )
 
-            for which in ("real", "imag"):
-                for w in range(WORDS):
-                    turned = []
-                    for e in range(2):
-                        bank = psum.tile([P, BANK], F32, tag="bank")
-                        for t in range(L_TILES):
-                            words = chunks[(which, t)][:].bitcast(F32).rearrange(
-                                "l (p j) -> l p j", j=2 * WORDS
+            def table(name):
+                return keep.tile([P, TILES * S], F32, name=name)
+
+            turns = table("turns")
+            nc.vector.tensor_scalar(
+                out=turns[:], in0=theta, scalar1=1.0 / (2.0 * math.pi), scalar2=ROUND_MAGIC,
+                op0=ALU.mult, op1=ALU.add,
+            )
+            nc.vector.tensor_scalar_sub(out=turns[:], in0=turns[:], scalar1=ROUND_MAGIC)
+            angle = table("angle")
+            nc.vector.scalar_tensor_tensor(
+                out=angle[:], in0=turns[:], scalar=-TWO_PI_HIGH, in1=theta,
+                op0=ALU.mult, op1=ALU.add,
+            )
+            nc.vector.scalar_tensor_tensor(
+                out=angle[:], in0=turns[:], scalar=-TWO_PI_LOW, in1=angle[:],
+                op0=ALU.mult, op1=ALU.add,
+            )
+            nc.vector.tensor_scalar(
+                out=angle[:], in0=angle[:], scalar1=-PI_BELOW, scalar2=PI_BELOW,
+                op0=ALU.max, op1=ALU.min,
+            )
+            sin_t = table("sin_t")
+            nc.scalar.activation(out=sin_t[:], in_=angle[:], func=ACT.Sin)
+            sin_half = table("sin_half")
+            nc.scalar.activation(out=sin_half[:], in_=angle[:], func=ACT.Sin, scale=0.5)
+            half_square = table("half_square")
+            nc.vector.tensor_tensor(
+                out=half_square[:], in0=sin_half[:], in1=sin_half[:], op=ALU.mult
+            )
+            cos_t = table("cos_t")
+            nc.vector.tensor_scalar(
+                out=cos_t[:], in0=half_square[:], scalar1=-2.0, scalar2=1.0,
+                op0=ALU.mult, op1=ALU.add,
+            )
+            early_root = keep.tile([P, 1], F32, name="early_root")
+            nc.scalar.activation(
+                out=early_root[:], in_=half_square[:, 0:1], func=ACT.Sqrt, bias=eps_column[:, 0:1]
+            )
+
+            def product(name, a, b):
+                result = table(name)
+                nc.vector.tensor_tensor(out=result[:], in0=a, in1=b, op=ALU.mult)
+                return result
+
+            coef = {"real": table("coef_real"), "imag": table("coef_imag")}
+            re_cos = product("re_cos", c_re, cos_t[:])
+            im_sin = product("im_sin", c_im, sin_t[:])
+            nc.vector.tensor_tensor(
+                out=coef["real"][:], in0=re_cos[:], in1=im_sin[:], op=ALU.subtract
+            )
+            re_sin = product("re_sin", c_re, sin_t[:])
+            im_cos = product("im_cos", c_im, cos_t[:])
+            nc.vector.scalar_tensor_tensor(
+                out=coef["imag"][:], in0=re_sin[:], scalar=-1.0, in1=im_cos[:],
+                op0=ALU.mult, op1=ALU.subtract,
+            )
+            re_re = product("re_re", c_re, b_re)
+            im_im = product("im_im", c_im, b_im)
+            nc.vector.tensor_tensor(out=re_re[:], in0=re_re[:], in1=im_im[:], op=ALU.subtract)
+            gain = keep.tile([P, TILES], F32, name="gain")
+            nc.vector.tensor_reduce(
+                out=gain[:], in_=re_re[:].rearrange("p (c s) -> p c s", s=S), axis=AXIS.X,
+                op=ALU.add,
+            )
+
+            all_words = [(which, w) for which in ("real", "imag") for w in range(WORDS)]
+            y_sums = {}
+            slow_sums = {}
+
+            def coefficient(which, q, e, w, h):
+                column = (2 * q + e) * S + 2 * w + h
+                return coef[which][:, column : column + 1]
+
+            def turn_word(chunks, which, w, ring):
+                views = []
+                for e in range(2):
+                    bank = psum.tile([P, BANK], F32, tag=ring)
+                    for t in range(L_TILES):
+                        words = chunks[(which, t)][:].bitcast(F32).rearrange(
+                            "l (p j) -> l p j", j=2 * WORDS
+                        )
+                        nc.tensor.transpose(
+                            bank[:, t * P : (t + 1) * P], words[:, :, WORDS * e + w], ident_f32[:]
+                        )
+                    views.append(bank[:].bitcast(BF16).rearrange("p (l h) -> p l h", h=2))
+                return views
+
+            def prepare(q):
+                g, u = divmod(q, 2)
+                w_raw, chunks = loaded[q]
+                quantise_weight_rows(w_raw[:], D // K_PASS, w1_codes, w1_scales, 256 * q)
+                if u == 0:
+                    y_sums[g] = sums.tile([P, 4, L], F32, tag="y_sum", name="y_sum")
+                y_pair = y_sums[g][:, 2 * u : 2 * u + 2, :]
+                for e in range(2):
+                    x_in = psum.tile([P, BANK], F32, tag="for_scalar")
+                    cols = slice(256 * q + P * e, 256 * q + P * (e + 1))
+                    for rows in (slice(0, 256), slice(256, L)):
+                        for c in range(D // K_PASS):
+                            nc.tensor.matmul_mx(
+                                out=x_in[:, rows],
+                                lhsT=w1_codes[:, c, cols].bitcast(FP8X4),
+                                lhsT_scale=w1_scales[:, c, cols],
+                                rhs=h_codes[:, c, rows].bitcast(FP8X4),
+                                rhs_scale=h_scales[:, c, rows],
+                                start=(c == 0),
+                                stop=(c == D // K_PASS - 1),
                             )
-                            nc.tensor.transpose(
-                                bank[:, t * P : (t + 1) * P], words[:, :, WORDS * e + w], ident_f32[:]
-                            )
-                        turned.append(bank[:].bitcast(BF16).rearrange("p (l h) -> p l h", h=2))
+                    nc.scalar.activation(
+                        out=y_pair[:, e, :], in_=x_in[:, 0:L], func=ACT.Copy,
+                        scale=gain[:, 2 * q + e : 2 * q + e + 1],
+                    )
+                slow_sums[q] = sums.tile([P, 2, L], F32, tag="slow_sum", name="slow_sum", bufs=3)
+                for n, (which, w) in enumerate(all_words[:SLOW_WORDS]):
+                    turned = turn_word(chunks, which, w, "for_scalar")
                     for h in range(2):
+                        first = n == 0 and h == 0
+                        if first:
+                            term = slow_sums[q]
+                        else:
+                            term = products.tile([P, 2, L], F32, tag="term")
                         for e in range(2):
-                            column = (2 * q + e) * S + 2 * w + h
+                            nc.scalar.activation(
+                                out=term[:, e, :], in_=turned[e][:, 0:L, h], func=ACT.Copy,
+                                scale=coefficient(which, q, e, w, h),
+                            )
+                        if not first:
+                            nc.gpsimd.tensor_tensor(
+                                out=slow_sums[q][:], in0=slow_sums[q][:], in1=term[:], op=ALU.add
+                            )
+
+            def add_fast_words(q):
+                g, u = divmod(q, 2)
+                chunks = loaded[q][1]
+                for which, w in all_words[SLOW_WORDS:]:
+                    turned = turn_word(chunks, which, w, "for_vector")
+                    for h in range(2):
+                        for e in (1, 0):
                             nc.vector.scalar_tensor_tensor(
-                                out=y_sum[:, 2 * u + e, :],
+                                out=y_sums[g][:, 2 * u + e, :],
                                 in0=turned[e][:, 0:L, h],
-                                scalar=coef[which][:, column : column + 1],
-                                in1=y_sum[:, 2 * u + e, :],
+                                scalar=coefficient(which, q, e, w, h),
+                                in1=y_sums[g][:, 2 * u + e, :],
                                 op0=ALU.mult,
                                 op1=ALU.add,
                             )
 
-            if u == 1:
-                quantise_weight_rows(w_out_raw[:], F // K_PASS, w2_codes, w2_scales, 256 * g)
-                for t in range(L_TILES):
-                    grouped_y = stage.tile([P, P, 4], BF16, tag="grouped_y", align_bytes=64)
-                    nc.scalar.copy(
-                        out=grouped_y[:],
-                        in_=y_sum[:, :, t * P : (t + 1) * P].rearrange("p k l -> p l k"),
-                    )
-                    nc.vector.quantize_mx(
-                        out=y_codes[:, g, t * P : (t + 1) * P].bitcast(FP8X4),
-                        scales=y_scales[:, g, t * P : (t + 1) * P],
-                        in_=grouped_y[:].rearrange("p l k -> p (l k)"),
-                    )
+            prepare(0)
+            for q in range(PAIRS):
+                g, u = divmod(q, 2)
+                if q + 2 < PAIRS:
+                    loaded[q + 2] = load_pair(q + 2)
+                if u == 1:
+                    w_out_raw = weights.tile([P, 2, F], BF16, tag="w_out_raw", bufs=1)
+                    nc.sync.dma_start(out=w_out_raw[:], in_=w_out_blocks[g])
+                    quantise_weight_rows(w_out_raw[:], F // K_PASS, w2_codes, w2_scales, 256 * g)
+                if q + 1 < PAIRS:
+                    prepare(q + 1)
+                add_fast_words(q)
+                y_pair = y_sums[g][:, 2 * u : 2 * u + 2, :]
+                nc.gpsimd.tensor_tensor(out=y_pair, in0=y_pair, in1=slow_sums[q][:], op=ALU.add)
+                if u == 1:
+                    for t in range(L_TILES):
+                        grouped_y = stage.tile([P, P, 4], BF16, tag="grouped_y", align_bytes=64)
+                        nc.scalar.copy(
+                            out=grouped_y[:],
+                            in_=y_sums[g][:, :, t * P : (t + 1) * P].rearrange("p k l -> p l k"),
+                        )
+                        nc.vector.quantize_mx(
+                            out=y_codes[:, g, t * P : (t + 1) * P].bitcast(FP8X4),
+                            scales=y_scales[:, g, t * P : (t + 1) * P],
+                            in_=grouped_y[:].rearrange("p l k -> p (l k)"),
+                        )
+            nc.sync.dma_start(out=mixer_rows[:], in_=mixer_norm_w.partition_broadcast(P))
+            nc.sync.dma_start(out=loop_rows[:], in_=loop_norm_w.partition_broadcast(P))
 
-        mixer_rows = keep.tile([P, D], BF16, name="mixer_rows")
-        nc.sync.dma_start(out=mixer_rows[:], in_=mixer_norm_w.partition_broadcast(P))
-        loop_rows = keep.tile([P, D], BF16, name="loop_rows")
-        nc.sync.dma_start(out=loop_rows[:], in_=loop_norm_w.partition_broadcast(P))
-        out_tiles = out.rearrange("b (t p) d -> (b t) p d", p=P)
-        HALVES = D // BANK
+        with ExitStack() as ending:
+            tail = ending.enter_context(tc.tile_pool(name="tail", bufs=2))
+            psum_tail = ending.enter_context(tc.psum_pool(name="psum_tail", bufs=6))
+            out_tiles = out.rearrange("b (t p) d -> (b t) p d", p=P)
+            halves = D // BANK
 
-        def inverse_rms(square_sums):
-            mean = tail.tile([P, 1], F32, tag="mean")
-            nc.vector.tensor_tensor(
-                out=mean[:], in0=square_sums[:, 0:1], in1=square_sums[:, 1:2], op=ALU.add
-            )
-            nc.vector.tensor_scalar(
-                out=mean[:], in0=mean[:], scalar1=1.0 / D, scalar2=EPS, op0=ALU.mult, op1=ALU.add
-            )
-            nc.scalar.sqrt(out=mean[:], in_=mean[:])
-            inverse = tail.tile([P, 1], F32, tag="inverse")
-            nc.vector.reciprocal(out=inverse[:], in_=mean[:])
-            return inverse
-
-        for t in range(L_TILES):
-            rows = slice(t * P, (t + 1) * P)
-            projected = []
-            proj_squares = tail.tile([P, HALVES], F32, tag="proj_squares")
-            for half in range(HALVES):
-                proj = psum.tile([P, BANK], F32, tag="bank")
-                for g in range(F // K_PASS):
-                    nc.tensor.matmul_mx(
-                        out=proj[:],
-                        lhsT=y_codes[:, g, rows].bitcast(FP8X4),
-                        lhsT_scale=y_scales[:, g, rows],
-                        rhs=w2_codes[:, g, half * BANK : (half + 1) * BANK].bitcast(FP8X4),
-                        rhs_scale=w2_scales[:, g, half * BANK : (half + 1) * BANK],
-                        start=(g == 0),
-                        stop=(g == F // K_PASS - 1),
-                    )
-                squared = tail.tile([P, BANK], F32, tag="squared")
+            def inverse_rms(square_sum):
+                root = tail.tile([P, 1], F32, tag="root")
                 nc.scalar.activation(
-                    out=squared[:], in_=proj[:], func=ACT.Square,
-                    accum_out=proj_squares[:, half : half + 1],
+                    out=root[:], in_=square_sum, func=ACT.Sqrt, bias=eps_column[:, 0:1],
+                    scale=1.0 / D,
                 )
-                projected.append(proj)
-            proj_scale = inverse_rms(proj_squares)
+                inverse = tail.tile([P, 1], F32, tag="inverse")
+                nc.vector.reciprocal(out=inverse[:], in_=root[:])
+                return inverse
 
-            residual = tail.tile([P, D], F32, tag="residual")
-            res_squares = tail.tile([P, HALVES], F32, tag="res_squares")
-            for half in range(HALVES):
-                cols = slice(half * BANK, (half + 1) * BANK)
-                nc.vector.scalar_tensor_tensor(
-                    out=residual[:, cols], in0=projected[half][:], scalar=proj_scale[:, 0:1],
-                    in1=mixer_rows[:, cols], op0=ALU.mult, op1=ALU.mult,
-                )
+            for t in range(L_TILES):
+                rows = slice(t * P, (t + 1) * P)
+                half_squares = tail.tile([P, halves], F32, tag="half_squares")
+                mixed = tail.tile([P, D], F32, tag="mixed")
+                for half in range(halves):
+                    cols = slice(half * BANK, (half + 1) * BANK)
+                    proj = psum_tail.tile([P, BANK], F32, tag="proj")
+                    for g in range(F // K_PASS):
+                        nc.tensor.matmul_mx(
+                            out=proj[:],
+                            lhsT=y_codes[:, g, rows].bitcast(FP8X4),
+                            lhsT_scale=y_scales[:, g, rows],
+                            rhs=w2_codes[:, g, cols].bitcast(FP8X4),
+                            rhs_scale=w2_scales[:, g, cols],
+                            start=(g == 0),
+                            stop=(g == F // K_PASS - 1),
+                        )
+                    nc.scalar.activation(
+                        out=mixed[:, cols], in_=proj[:], func=ACT.Square,
+                        accum_out=half_squares[:, half : half + 1],
+                    )
+                    nc.vector.tensor_tensor(
+                        out=mixed[:, cols], in0=proj[:], in1=mixer_rows[:, cols], op=ALU.mult
+                    )
+                proj_squares = tail.tile([P, 1], F32, tag="proj_squares")
                 nc.vector.tensor_tensor(
-                    out=residual[:, cols], in0=residual[:, cols], in1=h_f32[:, t, cols], op=ALU.add
+                    out=proj_squares[:], in0=half_squares[:, 0:1], in1=half_squares[:, 1:2],
+                    op=ALU.add,
                 )
-                squared = tail.tile([P, BANK], F32, tag="squared")
-                nc.scalar.activation(
-                    out=squared[:], in_=residual[:, cols], func=ACT.Square,
-                    accum_out=res_squares[:, half : half + 1],
-                )
-            res_scale = inverse_rms(res_squares)
+                proj_scale = inverse_rms(proj_squares[:])
 
-            result = tail.tile([P, D], F32, tag="result")
-            nc.vector.scalar_tensor_tensor(
-                out=result[:], in0=residual[:], scalar=res_scale[:, 0:1], in1=loop_rows[:],
-                op0=ALU.mult, op1=ALU.mult,
-            )
-            nc.sync.dma_start(out=out_tiles[t], in_=result[:])
+                residual = tail.tile([P, D], F32, tag="residual")
+                nc.vector.scalar_tensor_tensor(
+                    out=residual[:], in0=mixed[:], scalar=proj_scale[:, 0:1], in1=h_f32[:, t, :],
+                    op0=ALU.mult, op1=ALU.add,
+                )
+                squared = tail.tile([P, D], F32, tag="squared")
+                res_squares = tail.tile([P, 1], F32, tag="res_squares")
+                nc.scalar.activation(
+                    out=squared[:], in_=residual[:], func=ACT.Square, accum_out=res_squares[:]
+                )
+                result = tail.tile([P, D], F32, tag="result")
+                nc.vector.tensor_tensor(
+                    out=result[:], in0=residual[:], in1=loop_rows[:], op=ALU.mult
+                )
+                res_scale = inverse_rms(res_squares[:])
+                nc.vector.tensor_scalar_mul(out=result[:], in0=result[:], scalar1=res_scale[:, 0:1])
+                nc.sync.dma_start(out=out_tiles[t], in_=result[:])

@@ -339,10 +339,11 @@ def tile_recursivemamba130m_pa_kernel(
                 if u == 1:
                     w_out_raw = weights.tile([P, 2, F], BF16, tag="w_out_raw", bufs=1)
                     nc.sync.dma_start(out=w_out_raw[:], in_=w_out_blocks[g])
+                add_fast_words(q)
+                if u == 1:
                     quantise_weight_rows(w_out_raw[:], F // K_PASS, w2_codes, w2_scales, 256 * g)
                 if q + 1 < PAIRS:
                     prepare(q + 1)
-                add_fast_words(q)
                 y_pair = y_sums[g][:, 2 * u : 2 * u + 2, :]
                 nc.gpsimd.tensor_tensor(out=y_pair, in0=y_pair, in1=slow_sums[q][:], op=ALU.add)
                 if u == 1:

@@ -26,7 +26,12 @@ PAIRS = F // 256
 TILES = 2 * PAIRS
 WORDS = S // 2
 BANK = 512
-SLOW_WORDS = 2
+ALL_WORDS = [(which, w) for which in ("real", "imag") for w in range(WORDS)]
+SLOW_WORDS = ALL_WORDS[:2]
+FAST_WORDS = ALL_WORDS[2:]
+STEPS = len(FAST_WORDS)
+assert len(SLOW_WORDS) == 2 and STEPS == 6 and D // K_PASS == 2
+QUANTISE_LAG = 2
 
 ROUND_MAGIC = 12582912.0
 TWO_PI_HIGH = 6.28125
@@ -57,13 +62,6 @@ def tile_recursivemamba130m_pa_kernel(
     with ExitStack() as whole:
         keep = whole.enter_context(tc.tile_pool(name="keep", bufs=1))
 
-        ident_f32 = keep.tile([P, P], F32, name="ident_f32")
-        make_identity(nc, ident_f32[:])
-        ident_bf16 = keep.tile([P, P], BF16, name="ident_bf16")
-        make_identity(nc, ident_bf16[:])
-        eps_column = keep.tile([P, 1], F32, name="eps_column")
-        nc.vector.memset(eps_column[:], EPS)
-
         h_codes = keep.tile([P, D // K_PASS, L], U32, name="h_codes", align_bytes=64)
         h_scales = keep.tile([P, D // K_PASS, L], U8, name="h_scales", align_bytes=64)
         w1_codes = keep.tile([P, D // K_PASS, F], U32, name="w1_codes", align_bytes=64)
@@ -75,14 +73,22 @@ def tile_recursivemamba130m_pa_kernel(
         h_f32 = keep.tile([P, L_TILES, D], F32, name="h_f32")
         mixer_rows = keep.tile([P, D], BF16, name="mixer_rows")
         loop_rows = keep.tile([P, D], BF16, name="loop_rows")
+        eps_column = keep.tile([P, 1], F32, name="eps_column")
 
         with ExitStack() as body:
-            stream = body.enter_context(tc.tile_pool(name="stream", bufs=18))
+            stream = body.enter_context(tc.tile_pool(name="stream", bufs=12))
             weights = body.enter_context(tc.tile_pool(name="weights", bufs=2))
             stage = body.enter_context(tc.tile_pool(name="stage", bufs=3))
             sums = body.enter_context(tc.tile_pool(name="sums", bufs=2))
             products = body.enter_context(tc.tile_pool(name="products", bufs=4))
             psum = body.enter_context(tc.psum_pool(name="psum", bufs=4))
+            body.enter_context(tc.manual_schedule())
+
+            nc.vector.memset(eps_column[:], EPS)
+            ident_f32 = keep.tile([P, P], F32, name="ident_f32")
+            make_identity(nc, ident_f32[:])
+            ident_bf16 = keep.tile([P, P], BF16, name="ident_bf16")
+            make_identity(nc, ident_bf16[:])
 
             state_rows = {
                 "real": real.rearrange("b l c d s -> (b l) (c d s)"),
@@ -101,9 +107,12 @@ def tile_recursivemamba130m_pa_kernel(
                 )
                 return raw[:].rearrange("p q f -> p (q f)")
 
-            def load_pair(q):
+            def load_w_in(q):
                 w_raw = weights.tile([P, 2, D], BF16, tag="w_raw")
                 nc.sync.dma_start(out=w_raw[:], in_=w_in_pairs[q])
+                return w_raw
+
+            def load_state(q):
                 chunks = {}
                 for which in ("real", "imag"):
                     for t in range(L_TILES):
@@ -115,7 +124,7 @@ def tile_recursivemamba130m_pa_kernel(
                             ],
                         )
                         chunks[(which, t)] = chunk
-                return w_raw, chunks
+                return chunks
 
             x_sb = keep.tile([P, L_TILES, D], BF16, name="x_sb")
             nc.sync.dma_start(out=x_sb[:], in_=x.rearrange("b (t p) d -> p (b t) d", p=P))
@@ -126,59 +135,57 @@ def tile_recursivemamba130m_pa_kernel(
             c_im = load_table(C_imag, "c_im")
             b_re = load_table(B_real, "b_re")
             b_im = load_table(B_imag, "b_im")
-            loaded = {0: load_pair(0), 1: load_pair(1)}
+            w_raws = {0: load_w_in(0)}
+            states = {0: load_state(0)}
 
-            def quantise_weight_rows(raw, passes, codes, scales, col0):
+            waiting = {}
+
+            def quantise_waiting(step):
+                for grouped, codes, scales in waiting.get(step, []):
+                    nc.vector.quantize_mx(out=codes.bitcast(FP8X4), scales=scales, in_=grouped)
+
+            def turn_weight_pass(step, raw, g, codes, scales, col0):
                 raw_words = raw.bitcast(F32)
-                for g in range(passes):
-                    turned = psum.tile([P, BANK], F32, tag="for_scalar")
-                    for u in range(2):
-                        for i in range(2):
-                            first = 256 * g + 128 * u
-                            nc.tensor.transpose(
-                                turned[:, (2 * u + i) * P : (2 * u + i + 1) * P],
-                                raw_words[:, i, first : first + P],
-                                ident_f32[:],
-                            )
-                    grouped = stage.tile([P, 4 * 256], BF16, tag="grouped_w", align_bytes=64)
-                    nc.scalar.copy(
-                        out=grouped[:].bitcast(F32).rearrange("p (r u) -> p r u", u=2),
-                        in_=turned[:].rearrange("p (u r) -> p r u", u=2),
-                    )
-                    nc.vector.quantize_mx(
-                        out=codes[:, g, col0 : col0 + 256].bitcast(FP8X4),
-                        scales=scales[:, g, col0 : col0 + 256],
-                        in_=grouped[:],
-                    )
+                turned = psum.tile([P, BANK], F32, tag="for_scalar")
+                for u in range(2):
+                    for i in range(2):
+                        first = 256 * g + 128 * u
+                        nc.tensor.transpose(
+                            turned[:, (2 * u + i) * P : (2 * u + i + 1) * P],
+                            raw_words[:, i, first : first + P],
+                            ident_f32[:],
+                        )
+                grouped = stage.tile([P, 4 * 256], BF16, tag="grouped_w", bufs=6, align_bytes=64)
+                nc.scalar.copy(
+                    out=grouped[:].bitcast(F32).rearrange("p (r u) -> p r u", u=2),
+                    in_=turned[:].rearrange("p (u r) -> p r u", u=2),
+                )
+                waiting[step] = waiting.get(step, []) + [
+                    (grouped[:], codes[:, g, col0 : col0 + 256], scales[:, g, col0 : col0 + 256])
+                ]
+
+            def turn_word(q, which, w, ring):
+                views = []
+                for e in range(2):
+                    bank = psum.tile([P, BANK], F32, tag=ring)
+                    for t in range(L_TILES):
+                        words = states[q][(which, t)][:].bitcast(F32).rearrange(
+                            "l (p j) -> l p j", j=2 * WORDS
+                        )
+                        nc.tensor.transpose(
+                            bank[:, t * P : (t + 1) * P], words[:, :, WORDS * e + w], ident_f32[:]
+                        )
+                    views.append(bank[:].bitcast(BF16).rearrange("p (l h) -> p l h", h=2))
+                return views
+
+            early_sine = keep.tile([P, 1], F32, name="early_sine")
+            nc.scalar.activation(out=early_sine[:], in_=eps_column[:], func=ACT.Sin)
 
             h_bf16 = keep.tile([P, L_TILES, D], BF16, name="h_bf16")
             for t in range(L_TILES):
                 nc.vector.tensor_tensor(
                     out=h_bf16[:, t, :], in0=x_sb[:, t, :], in1=emb_rows[:], op=ALU.add
                 )
-                columns = h_bf16[:, t, :].rearrange("l (g u p e) -> l g u p e", g=2, u=2, e=2)
-                turned_h = psum.tile([P, 2 * BANK], BF16, tag="for_scalar")
-                for g in range(2):
-                    for u in range(2):
-                        for e in range(2):
-                            slot = 4 * g + 2 * u + e
-                            nc.tensor.transpose(
-                                turned_h[:, slot * P : (slot + 1) * P],
-                                columns[:, g, u, :, e],
-                                ident_bf16[:],
-                            )
-                grouped_h = stage.tile([P, 2, P, 4], BF16, tag="grouped_h", align_bytes=64)
-                nc.scalar.copy(
-                    out=grouped_h[:], in_=turned_h[:].rearrange("p (g k l) -> p g l k", g=2, k=4)
-                )
-                for g in range(2):
-                    nc.vector.quantize_mx(
-                        out=h_codes[:, g, t * P : (t + 1) * P].bitcast(FP8X4),
-                        scales=h_scales[:, g, t * P : (t + 1) * P],
-                        in_=grouped_h[:, g].rearrange("p l k -> p (l k)"),
-                    )
-
-            for t in range(L_TILES):
                 nc.gpsimd.tensor_tensor(
                     out=h_f32[:, t, :], in0=x_sb[:, t, :], in1=emb_rows[:], op=ALU.add
                 )
@@ -209,18 +216,30 @@ def tile_recursivemamba130m_pa_kernel(
             nc.scalar.activation(out=sin_t[:], in_=angle[:], func=ACT.Sin)
             sin_half = table("sin_half")
             nc.scalar.activation(out=sin_half[:], in_=angle[:], func=ACT.Sin, scale=0.5)
-            half_square = table("half_square")
-            nc.vector.tensor_tensor(
-                out=half_square[:], in0=sin_half[:], in1=sin_half[:], op=ALU.mult
-            )
+
+            grouped_hs = []
+            for t in range(L_TILES):
+                columns = h_bf16[:, t, :].rearrange("l (g u p e) -> l g u p e", g=2, u=2, e=2)
+                turned_h = psum.tile([P, 2 * BANK], BF16, tag="for_scalar")
+                for g in range(2):
+                    for u in range(2):
+                        for e in range(2):
+                            slot = 4 * g + 2 * u + e
+                            nc.tensor.transpose(
+                                turned_h[:, slot * P : (slot + 1) * P],
+                                columns[:, g, u, :, e],
+                                ident_bf16[:],
+                            )
+                grouped_h = stage.tile([P, 2, P, 4], BF16, tag="grouped_h", align_bytes=64)
+                nc.scalar.copy(
+                    out=grouped_h[:], in_=turned_h[:].rearrange("p (g k l) -> p g l k", g=2, k=4)
+                )
+                grouped_hs.append(grouped_h)
+
             cos_t = table("cos_t")
+            nc.vector.tensor_tensor(out=cos_t[:], in0=sin_half[:], in1=sin_half[:], op=ALU.mult)
             nc.vector.tensor_scalar(
-                out=cos_t[:], in0=half_square[:], scalar1=-2.0, scalar2=1.0,
-                op0=ALU.mult, op1=ALU.add,
-            )
-            early_root = keep.tile([P, 1], F32, name="early_root")
-            nc.scalar.activation(
-                out=early_root[:], in_=half_square[:, 0:1], func=ACT.Sqrt, bias=eps_column[:, 0:1]
+                out=cos_t[:], in0=cos_t[:], scalar1=-2.0, scalar2=1.0, op0=ALU.mult, op1=ALU.add
             )
 
             def product(name, a, b):
@@ -248,116 +267,155 @@ def tile_recursivemamba130m_pa_kernel(
                 out=gain[:], in_=re_re[:].rearrange("p (c s) -> p c s", s=S), axis=AXIS.X,
                 op=ALU.add,
             )
+            for t in range(L_TILES):
+                for g in range(2):
+                    nc.vector.quantize_mx(
+                        out=h_codes[:, g, t * P : (t + 1) * P].bitcast(FP8X4),
+                        scales=h_scales[:, g, t * P : (t + 1) * P],
+                        in_=grouped_hs[t][:, g].rearrange("p l k -> p (l k)"),
+                    )
+            for c in range(D // K_PASS):
+                turn_weight_pass(c - QUANTISE_LAG, w_raws[0][:], c, w1_codes, w1_scales, 0)
 
-            all_words = [(which, w) for which in ("real", "imag") for w in range(WORDS)]
             y_sums = {}
             slow_sums = {}
+            w_out_raws = {}
 
             def coefficient(which, q, e, w, h):
                 column = (2 * q + e) * S + 2 * w + h
                 return coef[which][:, column : column + 1]
 
-            def turn_word(chunks, which, w, ring):
-                views = []
-                for e in range(2):
-                    bank = psum.tile([P, BANK], F32, tag=ring)
-                    for t in range(L_TILES):
-                        words = chunks[(which, t)][:].bitcast(F32).rearrange(
-                            "l (p j) -> l p j", j=2 * WORDS
+            def add_slow_word(q, index):
+                which, w = SLOW_WORDS[index]
+                turned = turn_word(q, which, w, "for_scalar")
+                for h in range(2):
+                    first = index == 0 and h == 0
+                    if first:
+                        slow_sums[q] = sums.tile([P, 2, L], F32, tag="slow_sum", name="slow_sum")
+                        term = slow_sums[q]
+                    else:
+                        term = products.tile([P, 2, L], F32, tag="term")
+                    for e in range(2):
+                        nc.scalar.activation(
+                            out=term[:, e, :], in_=turned[e][:, 0:L, h], func=ACT.Copy,
+                            scale=coefficient(which, q, e, w, h),
                         )
-                        nc.tensor.transpose(
-                            bank[:, t * P : (t + 1) * P], words[:, :, WORDS * e + w], ident_f32[:]
+                    if not first:
+                        nc.gpsimd.tensor_tensor(
+                            out=slow_sums[q][:], in0=slow_sums[q][:], in1=term[:], op=ALU.add
                         )
-                    views.append(bank[:].bitcast(BF16).rearrange("p (l h) -> p l h", h=2))
-                return views
 
-            def prepare(q):
+            def project_in(q, e, term):
+                x_in = psum.tile([P, BANK], F32, tag="for_scalar")
+                cols = slice(256 * q + P * e, 256 * q + P * (e + 1))
+                for rows in (slice(0, 256), slice(256, L)):
+                    for c in range(D // K_PASS):
+                        nc.tensor.matmul_mx(
+                            out=x_in[:, rows],
+                            lhsT=w1_codes[:, c, cols].bitcast(FP8X4),
+                            lhsT_scale=w1_scales[:, c, cols],
+                            rhs=h_codes[:, c, rows].bitcast(FP8X4),
+                            rhs_scale=h_scales[:, c, rows],
+                            start=(c == 0),
+                            stop=(c == D // K_PASS - 1),
+                        )
+                nc.scalar.activation(
+                    out=term[:, e, :], in_=x_in[:, 0:L], func=ACT.Copy,
+                    scale=gain[:, 2 * q + e : 2 * q + e + 1],
+                )
+
+            def add_fast_word(q, j, turned):
                 g, u = divmod(q, 2)
-                w_raw, chunks = loaded[q]
-                quantise_weight_rows(w_raw[:], D // K_PASS, w1_codes, w1_scales, 256 * q)
-                if u == 0:
-                    y_sums[g] = sums.tile([P, 4, L], F32, tag="y_sum", name="y_sum")
-                y_pair = y_sums[g][:, 2 * u : 2 * u + 2, :]
-                for e in range(2):
-                    x_in = psum.tile([P, BANK], F32, tag="for_scalar")
-                    cols = slice(256 * q + P * e, 256 * q + P * (e + 1))
-                    for rows in (slice(0, 256), slice(256, L)):
-                        for c in range(D // K_PASS):
-                            nc.tensor.matmul_mx(
-                                out=x_in[:, rows],
-                                lhsT=w1_codes[:, c, cols].bitcast(FP8X4),
-                                lhsT_scale=w1_scales[:, c, cols],
-                                rhs=h_codes[:, c, rows].bitcast(FP8X4),
-                                rhs_scale=h_scales[:, c, rows],
-                                start=(c == 0),
-                                stop=(c == D // K_PASS - 1),
+                which, w = FAST_WORDS[j]
+                for h in range(2):
+                    for e in (1, 0):
+                        y_tile = y_sums[g][:, 2 * u + e, :]
+                        if j == 0 and h == 0:
+                            nc.vector.tensor_scalar_mul(
+                                out=y_tile, in0=turned[e][:, 0:L, h],
+                                scalar1=coefficient(which, q, e, w, h),
                             )
-                    nc.scalar.activation(
-                        out=y_pair[:, e, :], in_=x_in[:, 0:L], func=ACT.Copy,
-                        scale=gain[:, 2 * q + e : 2 * q + e + 1],
-                    )
-                slow_sums[q] = sums.tile([P, 2, L], F32, tag="slow_sum", name="slow_sum", bufs=3)
-                for n, (which, w) in enumerate(all_words[:SLOW_WORDS]):
-                    turned = turn_word(chunks, which, w, "for_scalar")
-                    for h in range(2):
-                        first = n == 0 and h == 0
-                        if first:
-                            term = slow_sums[q]
                         else:
-                            term = products.tile([P, 2, L], F32, tag="term")
-                        for e in range(2):
-                            nc.scalar.activation(
-                                out=term[:, e, :], in_=turned[e][:, 0:L, h], func=ACT.Copy,
-                                scale=coefficient(which, q, e, w, h),
-                            )
-                        if not first:
-                            nc.gpsimd.tensor_tensor(
-                                out=slow_sums[q][:], in0=slow_sums[q][:], in1=term[:], op=ALU.add
-                            )
-
-            def add_fast_words(q):
-                g, u = divmod(q, 2)
-                chunks = loaded[q][1]
-                for which, w in all_words[SLOW_WORDS:]:
-                    turned = turn_word(chunks, which, w, "for_vector")
-                    for h in range(2):
-                        for e in (1, 0):
                             nc.vector.scalar_tensor_tensor(
-                                out=y_sums[g][:, 2 * u + e, :],
-                                in0=turned[e][:, 0:L, h],
-                                scalar=coefficient(which, q, e, w, h),
-                                in1=y_sums[g][:, 2 * u + e, :],
-                                op0=ALU.mult,
-                                op1=ALU.add,
+                                out=y_tile, in0=turned[e][:, 0:L, h],
+                                scalar=coefficient(which, q, e, w, h), in1=y_tile,
+                                op0=ALU.mult, op1=ALU.add,
                             )
 
-            prepare(0)
-            for q in range(PAIRS):
+            def round_pass(step, g):
+                for t in range(L_TILES):
+                    grouped_y = stage.tile([P, P, 4], BF16, tag="grouped_y", align_bytes=64)
+                    nc.scalar.copy(
+                        out=grouped_y[:],
+                        in_=y_sums[g][:, :, t * P : (t + 1) * P].rearrange("p k l -> p l k"),
+                    )
+                    waiting[step] = waiting.get(step, []) + [
+                        (
+                            grouped_y[:].rearrange("p l k -> p (l k)"),
+                            y_codes[:, g, t * P : (t + 1) * P],
+                            y_scales[:, g, t * P : (t + 1) * P],
+                        )
+                    ]
+
+            steps = [(q, j) for q in range(PAIRS) for j in range(STEPS)]
+            turned_next = turn_word(0, FAST_WORDS[0][0], FAST_WORDS[0][1], "for_vector")
+            for step, (q, j) in enumerate(steps):
                 g, u = divmod(q, 2)
-                if q + 2 < PAIRS:
-                    loaded[q + 2] = load_pair(q + 2)
-                if u == 1:
-                    w_out_raw = weights.tile([P, 2, F], BF16, tag="w_out_raw", bufs=1)
-                    nc.sync.dma_start(out=w_out_raw[:], in_=w_out_blocks[g])
-                add_fast_words(q)
-                if u == 1:
-                    quantise_weight_rows(w_out_raw[:], F // K_PASS, w2_codes, w2_scales, 256 * g)
-                if q + 1 < PAIRS:
-                    prepare(q + 1)
-                y_pair = y_sums[g][:, 2 * u : 2 * u + 2, :]
-                nc.gpsimd.tensor_tensor(out=y_pair, in0=y_pair, in1=slow_sums[q][:], op=ALU.add)
-                if u == 1:
-                    for t in range(L_TILES):
-                        grouped_y = stage.tile([P, P, 4], BF16, tag="grouped_y", align_bytes=64)
-                        nc.scalar.copy(
-                            out=grouped_y[:],
-                            in_=y_sums[g][:, :, t * P : (t + 1) * P].rearrange("p k l -> p l k"),
+                if j == 0:
+                    if u == 0:
+                        y_sums[g] = sums.tile([P, 4, L], F32, tag="y_sum", name="y_sum")
+                        w_out_raws[g] = weights.tile(
+                            [P, 2, F], BF16, tag="w_out_raw", name="w_out_raw"
                         )
-                        nc.vector.quantize_mx(
-                            out=y_codes[:, g, t * P : (t + 1) * P].bitcast(FP8X4),
-                            scales=y_scales[:, g, t * P : (t + 1) * P],
-                            in_=grouped_y[:].rearrange("p l k -> p (l k)"),
+                        nc.sync.dma_start(out=w_out_raws[g][:], in_=w_out_blocks[g])
+                    if q + 1 < PAIRS:
+                        w_raws[q + 1] = load_w_in(q + 1)
+                        states[q + 1] = load_state(q + 1)
+
+                turned = turned_next
+                if step + 1 < len(steps):
+                    next_q, next_j = steps[step + 1]
+                    turned_next = turn_word(
+                        next_q, FAST_WORDS[next_j][0], FAST_WORDS[next_j][1], "for_vector"
+                    )
+
+                if j < 2:
+                    add_slow_word(q, j)
+                elif j < 4:
+                    e = j - 2
+                    if e == 0:
+                        x_term = products.tile([P, 2, L], F32, tag="term")
+                        if u == 0 and g > 0:
+                            round_pass(step, g - 1)
+                    project_in(q, e, x_term)
+                    if e == 1:
+                        nc.gpsimd.tensor_tensor(
+                            out=slow_sums[q][:], in0=slow_sums[q][:], in1=x_term[:], op=ALU.add
                         )
+                else:
+                    c = j - 4
+                    if q + 1 < PAIRS:
+                        turn_weight_pass(
+                            step, w_raws[q + 1][:], c, w1_codes, w1_scales, 256 * (q + 1)
+                        )
+                    turn_weight_pass(
+                        step, w_out_raws[g][:], 2 * u + c, w2_codes, w2_scales, 256 * g
+                    )
+
+                quantise_waiting(step - QUANTISE_LAG)
+                add_fast_word(q, j, turned)
+                if j == STEPS - 1:
+                    y_pair = y_sums[g][:, 2 * u : 2 * u + 2, :]
+                    nc.gpsimd.tensor_tensor(
+                        out=y_pair, in0=y_pair, in1=slow_sums[q][:], op=ALU.add
+                    )
+
+            for step in range(len(steps), len(steps) + QUANTISE_LAG):
+                quantise_waiting(step - QUANTISE_LAG)
+            early_root = keep.tile([P, 1], F32, name="early_root")
+            nc.scalar.activation(out=early_root[:], in_=eps_column[:], func=ACT.Sqrt)
+            round_pass(len(steps), F // K_PASS - 1)
+            quantise_waiting(len(steps))
             nc.sync.dma_start(out=mixer_rows[:], in_=mixer_norm_w.partition_broadcast(P))
             nc.sync.dma_start(out=loop_rows[:], in_=loop_norm_w.partition_broadcast(P))
 

@@ -324,23 +324,28 @@ def tile_recursivemamba130m_pa_kernel(
                     scale=gain[:, 2 * q + e : 2 * q + e + 1],
                 )
 
+            def start_sums(q, turned):
+                g, u = divmod(q, 2)
+                which, w = FAST_WORDS[0]
+                if u == 0:
+                    y_sums[g] = sums.tile([P, 4, L], F32, tag="y_sum", name="y_sum")
+                for e in range(2):
+                    nc.scalar.activation(
+                        out=y_sums[g][:, 2 * u + e, :], in_=turned[e][:, 0:L, 0], func=ACT.Copy,
+                        scale=coefficient(which, q, e, w, 0),
+                    )
+
             def add_fast_word(q, j, turned):
                 g, u = divmod(q, 2)
                 which, w = FAST_WORDS[j]
-                for h in range(2):
+                for h in (1,) if j == 0 else (0, 1):
                     for e in (1, 0):
                         y_tile = y_sums[g][:, 2 * u + e, :]
-                        if j == 0 and h == 0:
-                            nc.vector.tensor_scalar_mul(
-                                out=y_tile, in0=turned[e][:, 0:L, h],
-                                scalar1=coefficient(which, q, e, w, h),
-                            )
-                        else:
-                            nc.vector.scalar_tensor_tensor(
-                                out=y_tile, in0=turned[e][:, 0:L, h],
-                                scalar=coefficient(which, q, e, w, h), in1=y_tile,
-                                op0=ALU.mult, op1=ALU.add,
-                            )
+                        nc.vector.scalar_tensor_tensor(
+                            out=y_tile, in0=turned[e][:, 0:L, h],
+                            scalar=coefficient(which, q, e, w, h), in1=y_tile,
+                            op0=ALU.mult, op1=ALU.add,
+                        )
 
             def round_pass(step, g):
                 for t in range(L_TILES):
@@ -359,11 +364,11 @@ def tile_recursivemamba130m_pa_kernel(
 
             steps = [(q, j) for q in range(PAIRS) for j in range(STEPS)]
             turned_next = turn_word(0, FAST_WORDS[0][0], FAST_WORDS[0][1], "for_vector")
+            start_sums(0, turned_next)
             for step, (q, j) in enumerate(steps):
                 g, u = divmod(q, 2)
                 if j == 0:
                     if u == 0:
-                        y_sums[g] = sums.tile([P, 4, L], F32, tag="y_sum", name="y_sum")
                         w_out_raws[g] = weights.tile(
                             [P, 2, F], BF16, tag="w_out_raw", name="w_out_raw"
                         )
@@ -378,6 +383,8 @@ def tile_recursivemamba130m_pa_kernel(
                     turned_next = turn_word(
                         next_q, FAST_WORDS[next_j][0], FAST_WORDS[next_j][1], "for_vector"
                     )
+                    if next_j == 0:
+                        start_sums(next_q, turned_next)
 
                 if j < 2:
                     add_slow_word(q, j)
@@ -405,10 +412,12 @@ def tile_recursivemamba130m_pa_kernel(
                 quantise_waiting(step - QUANTISE_LAG)
                 add_fast_word(q, j, turned)
                 if j == STEPS - 1:
-                    y_pair = y_sums[g][:, 2 * u : 2 * u + 2, :]
-                    nc.gpsimd.tensor_tensor(
-                        out=y_pair, in0=y_pair, in1=slow_sums[q][:], op=ALU.add
-                    )
+                    for t in range(L_TILES):
+                        rows = slice(t * P, (t + 1) * P)
+                        y_block = y_sums[g][:, 2 * u : 2 * u + 2, rows]
+                        nc.gpsimd.tensor_tensor(
+                            out=y_block, in0=y_block, in1=slow_sums[q][:, :, rows], op=ALU.add
+                        )
 
             for step in range(len(steps), len(steps) + QUANTISE_LAG):
                 quantise_waiting(step - QUANTISE_LAG)
@@ -477,7 +486,7 @@ def tile_recursivemamba130m_pa_kernel(
                     out=squared[:], in_=residual[:], func=ACT.Square, accum_out=res_squares[:]
                 )
                 result = tail.tile([P, D], F32, tag="result")
-                nc.vector.tensor_tensor(
+                nc.gpsimd.tensor_tensor(
                     out=result[:], in0=residual[:], in1=loop_rows[:], op=ALU.mult
                 )
                 res_scale = inverse_rms(res_squares[:])

@@ -11,7 +11,6 @@ U8 = mybir.dt.uint8
 FP8X4 = mybir.dt.float8_e4m3fn_x4
 ALU = mybir.AluOpType
 ACT = mybir.ActivationFunctionType
-AXIS = mybir.AxisListType
 
 P = 128
 L = 384
@@ -22,15 +21,19 @@ EPS = 1e-6
 
 L_TILES = L // P
 K_PASS = 512
+IN_PASSES = D // K_PASS
+OUT_PASSES = F // K_PASS
 PAIRS = F // 256
 TILES = 2 * PAIRS
 WORDS = S // 2
 BANK = 512
+HALVES = D // BANK
+RING = 4
 ALL_WORDS = [(which, w) for which in ("real", "imag") for w in range(WORDS)]
 SLOW_WORDS = ALL_WORDS[:2]
 FAST_WORDS = ALL_WORDS[2:]
 STEPS = len(FAST_WORDS)
-assert len(SLOW_WORDS) == 2 and STEPS == 6 and D // K_PASS == 2
+assert len(SLOW_WORDS) == 2 and STEPS == 6 and IN_PASSES == 2
 QUANTISE_LAG = 2
 
 ROUND_MAGIC = 12582912.0
@@ -61,30 +64,71 @@ def tile_recursivemamba130m_pa_kernel(
     nc = tc.nc
     with ExitStack() as whole:
         keep = whole.enter_context(tc.tile_pool(name="keep", bufs=1))
+        psum = whole.enter_context(tc.psum_pool(name="psum", bufs=RING))
+        stage = whole.enter_context(tc.tile_pool(name="stage", bufs=3))
+        sums = whole.enter_context(tc.tile_pool(name="sums", bufs=2))
+        whole.enter_context(tc.manual_schedule())
 
-        h_codes = keep.tile([P, D // K_PASS, L], U32, name="h_codes", align_bytes=64)
-        h_scales = keep.tile([P, D // K_PASS, L], U8, name="h_scales", align_bytes=64)
-        w1_codes = keep.tile([P, D // K_PASS, F], U32, name="w1_codes", align_bytes=64)
-        w1_scales = keep.tile([P, D // K_PASS, F], U8, name="w1_scales", align_bytes=64)
-        y_codes = keep.tile([P, F // K_PASS, L], U32, name="y_codes", align_bytes=64)
-        y_scales = keep.tile([P, F // K_PASS, L], U8, name="y_scales", align_bytes=64)
-        w2_codes = keep.tile([P, F // K_PASS, D], U32, name="w2_codes", align_bytes=64)
-        w2_scales = keep.tile([P, F // K_PASS, D], U8, name="w2_scales", align_bytes=64)
+        h_codes = keep.tile([P, IN_PASSES, L], U32, name="h_codes", align_bytes=64)
+        h_scales = keep.tile([P, IN_PASSES, L], U8, name="h_scales", align_bytes=64)
+        w1_codes = keep.tile([P, IN_PASSES, F], U32, name="w1_codes", align_bytes=64)
+        w1_scales = keep.tile([P, IN_PASSES, F], U8, name="w1_scales", align_bytes=64)
+        y_codes = keep.tile([P, OUT_PASSES, L], U32, name="y_codes", align_bytes=64)
+        y_scales = keep.tile([P, OUT_PASSES, L], U8, name="y_scales", align_bytes=64)
+        w2_codes = keep.tile([P, OUT_PASSES, D], U32, name="w2_codes", align_bytes=64)
+        w2_scales = keep.tile([P, OUT_PASSES, D], U8, name="w2_scales", align_bytes=64)
         h_f32 = keep.tile([P, L_TILES, D], F32, name="h_f32")
+        emb_rows = keep.tile([P, D], BF16, name="emb_rows")
         mixer_rows = keep.tile([P, D], BF16, name="mixer_rows")
         loop_rows = keep.tile([P, D], BF16, name="loop_rows")
         eps_column = keep.tile([P, 1], F32, name="eps_column")
+        y_sums = {}
+        projections = {}
+        waiting = {}
+
+        def quantise_later(step, grouped, codes, scales):
+            waiting[step] = waiting.get(step, []) + [(grouped, codes, scales)]
+
+        def quantise_waiting(last_step):
+            for step in sorted(waiting):
+                if step <= last_step:
+                    for grouped, codes, scales in waiting[step]:
+                        nc.vector.quantize_mx(out=codes.bitcast(FP8X4), scales=scales, in_=grouped)
+                    waiting[step] = []
+
+        def round_block(step, g, t):
+            rows = slice(t * P, (t + 1) * P)
+            grouped_y = stage.tile([P, P, 4], BF16, tag="grouped_y", align_bytes=64)
+            nc.scalar.copy(out=grouped_y[:], in_=y_sums[g][:, :, rows].rearrange("p k l -> p l k"))
+            quantise_later(
+                step, grouped_y[:].rearrange("p l k -> p (l k)"), y_codes[:, g, rows],
+                y_scales[:, g, rows],
+            )
+
+        def project_out(t, half, passes):
+            rows = slice(t * P, (t + 1) * P)
+            cols = slice(half * BANK, (half + 1) * BANK)
+            for g in passes:
+                nc.tensor.matmul_mx(
+                    out=projections[(t, half)][:],
+                    lhsT=y_codes[:, g, rows].bitcast(FP8X4),
+                    lhsT_scale=y_scales[:, g, rows],
+                    rhs=w2_codes[:, g, cols].bitcast(FP8X4),
+                    rhs_scale=w2_scales[:, g, cols],
+                    start=(g == 0),
+                    stop=(g == OUT_PASSES - 1),
+                )
 
         with ExitStack() as body:
             stream = body.enter_context(tc.tile_pool(name="stream", bufs=12))
             weights = body.enter_context(tc.tile_pool(name="weights", bufs=2))
-            stage = body.enter_context(tc.tile_pool(name="stage", bufs=3))
-            sums = body.enter_context(tc.tile_pool(name="sums", bufs=2))
             products = body.enter_context(tc.tile_pool(name="products", bufs=4))
-            psum = body.enter_context(tc.psum_pool(name="psum", bufs=4))
-            body.enter_context(tc.manual_schedule())
 
             nc.vector.memset(eps_column[:], EPS)
+            emb_alone = keep.tile([P, D], BF16, name="emb_alone")
+            nc.vector.memset(emb_alone[:], 0.0)
+            ones = keep.tile([P, P], BF16, name="ones")
+            nc.vector.memset(ones[:], 1.0)
             ident_f32 = keep.tile([P, P], F32, name="ident_f32")
             make_identity(nc, ident_f32[:])
             ident_bf16 = keep.tile([P, P], BF16, name="ident_bf16")
@@ -96,6 +140,7 @@ def tile_recursivemamba130m_pa_kernel(
             }
             w_in_pairs = w_in.rearrange("(q p e) k -> q p e k", p=P, e=2)
             w_out_blocks = out_proj_w.rearrange("(r i p) k -> r p i k", i=2, p=P)
+            states = {}
 
             def load_table(table, name):
                 raw = keep.tile([P, PAIRS, 2 * S], BF16, name=name)
@@ -112,37 +157,28 @@ def tile_recursivemamba130m_pa_kernel(
                 nc.sync.dma_start(out=w_raw[:], in_=w_in_pairs[q])
                 return w_raw
 
-            def load_state(q):
-                chunks = {}
-                for which in ("real", "imag"):
-                    for t in range(L_TILES):
-                        chunk = stream.tile([P, 256 * S], BF16, tag="chunk")
-                        nc.sync.dma_start(
-                            out=chunk[:],
-                            in_=state_rows[which][
-                                t * P : (t + 1) * P, q * 256 * S : (q + 1) * 256 * S
-                            ],
-                        )
-                        chunks[(which, t)] = chunk
-                return chunks
+            def load_state(q, which):
+                for t in range(L_TILES):
+                    chunk = stream.tile([P, 256 * S], BF16, tag="chunk")
+                    nc.sync.dma_start(
+                        out=chunk[:],
+                        in_=state_rows[which][
+                            t * P : (t + 1) * P, q * 256 * S : (q + 1) * 256 * S
+                        ],
+                    )
+                    states[(q, which, t)] = chunk
 
+            nc.sync.dma_start(out=emb_alone[0:1, :], in_=step_emb.rearrange("(o d) -> o d", o=1))
             x_sb = keep.tile([P, L_TILES, D], BF16, name="x_sb")
             nc.sync.dma_start(out=x_sb[:], in_=x.rearrange("b (t p) d -> p (b t) d", p=P))
-            emb_rows = keep.tile([P, D], BF16, name="emb_rows")
-            nc.sync.dma_start(out=emb_rows[:], in_=step_emb.partition_broadcast(P))
             theta = load_table(A_theta, "theta")
             c_re = load_table(C_real, "c_re")
             c_im = load_table(C_imag, "c_im")
+            load_state(0, "real")
+            w_raws = {0: load_w_in(0)}
             b_re = load_table(B_real, "b_re")
             b_im = load_table(B_imag, "b_im")
-            w_raws = {0: load_w_in(0)}
-            states = {0: load_state(0)}
-
-            waiting = {}
-
-            def quantise_waiting(step):
-                for grouped, codes, scales in waiting.get(step, []):
-                    nc.vector.quantize_mx(out=codes.bitcast(FP8X4), scales=scales, in_=grouped)
+            load_state(0, "imag")
 
             def turn_weight_pass(step, raw, g, codes, scales, col0):
                 raw_words = raw.bitcast(F32)
@@ -160,16 +196,16 @@ def tile_recursivemamba130m_pa_kernel(
                     out=grouped[:].bitcast(F32).rearrange("p (r u) -> p r u", u=2),
                     in_=turned[:].rearrange("p (u r) -> p r u", u=2),
                 )
-                waiting[step] = waiting.get(step, []) + [
-                    (grouped[:], codes[:, g, col0 : col0 + 256], scales[:, g, col0 : col0 + 256])
-                ]
+                quantise_later(
+                    step, grouped[:], codes[:, g, col0 : col0 + 256], scales[:, g, col0 : col0 + 256]
+                )
 
             def turn_word(q, which, w, ring):
                 views = []
                 for e in range(2):
                     bank = psum.tile([P, BANK], F32, tag=ring)
                     for t in range(L_TILES):
-                        words = states[q][(which, t)][:].bitcast(F32).rearrange(
+                        words = states[(q, which, t)][:].bitcast(F32).rearrange(
                             "l (p j) -> l p j", j=2 * WORDS
                         )
                         nc.tensor.transpose(
@@ -181,13 +217,18 @@ def tile_recursivemamba130m_pa_kernel(
             early_sine = keep.tile([P, 1], F32, name="early_sine")
             nc.scalar.activation(out=early_sine[:], in_=eps_column[:], func=ACT.Sin)
 
+            for half in range(HALVES):
+                cols = slice(half * BANK, (half + 1) * BANK)
+                spread = psum.tile([P, BANK], F32, tag="for_scalar")
+                nc.tensor.matmul(
+                    out=spread[:], lhsT=ones[:], rhs=emb_alone[:, cols], start=True, stop=True
+                )
+                nc.scalar.copy(out=emb_rows[:, cols], in_=spread[:])
+
             h_bf16 = keep.tile([P, L_TILES, D], BF16, name="h_bf16")
             for t in range(L_TILES):
                 nc.vector.tensor_tensor(
                     out=h_bf16[:, t, :], in0=x_sb[:, t, :], in1=emb_rows[:], op=ALU.add
-                )
-                nc.gpsimd.tensor_tensor(
-                    out=h_f32[:, t, :], in0=x_sb[:, t, :], in1=emb_rows[:], op=ALU.add
                 )
 
             def table(name):
@@ -212,16 +253,31 @@ def tile_recursivemamba130m_pa_kernel(
                 out=angle[:], in0=angle[:], scalar1=-PI_BELOW, scalar2=PI_BELOW,
                 op0=ALU.max, op1=ALU.min,
             )
-            sin_t = table("sin_t")
-            nc.scalar.activation(out=sin_t[:], in_=angle[:], func=ACT.Sin)
+            minus_sin = table("minus_sin")
+            nc.scalar.activation(out=minus_sin[:], in_=angle[:], func=ACT.Sin, scale=-1.0)
             sin_half = table("sin_half")
             nc.scalar.activation(out=sin_half[:], in_=angle[:], func=ACT.Sin, scale=0.5)
 
-            grouped_hs = []
+            def product(engine, name, a, b):
+                result = table(name)
+                engine.tensor_tensor(out=result[:], in0=a, in1=b, op=ALU.mult)
+                return result
+
+            coef = {"real": table("coef_real"), "imag": table("coef_imag")}
+            cos_t = product(nc.vector, "cos_t", sin_half[:], sin_half[:])
+            im_sin = product(nc.vector, "im_sin", c_im, minus_sin[:])
+            nc.vector.tensor_scalar(
+                out=cos_t[:], in0=cos_t[:], scalar1=-2.0, scalar2=1.0, op0=ALU.mult, op1=ALU.add
+            )
+            re_cos = product(nc.vector, "re_cos", c_re, cos_t[:])
+            nc.vector.tensor_tensor(
+                out=coef["real"][:], in0=re_cos[:], in1=im_sin[:], op=ALU.add
+            )
+
             for t in range(L_TILES):
                 columns = h_bf16[:, t, :].rearrange("l (g u p e) -> l g u p e", g=2, u=2, e=2)
                 turned_h = psum.tile([P, 2 * BANK], BF16, tag="for_scalar")
-                for g in range(2):
+                for g in range(IN_PASSES):
                     for u in range(2):
                         for e in range(2):
                             slot = 4 * g + 2 * u + e
@@ -230,54 +286,37 @@ def tile_recursivemamba130m_pa_kernel(
                                 columns[:, g, u, :, e],
                                 ident_bf16[:],
                             )
-                grouped_h = stage.tile([P, 2, P, 4], BF16, tag="grouped_h", align_bytes=64)
+                grouped_h = stage.tile([P, IN_PASSES, P, 4], BF16, tag="grouped_h", align_bytes=64)
                 nc.scalar.copy(
                     out=grouped_h[:], in_=turned_h[:].rearrange("p (g k l) -> p g l k", g=2, k=4)
                 )
-                grouped_hs.append(grouped_h)
-
-            cos_t = table("cos_t")
-            nc.vector.tensor_tensor(out=cos_t[:], in0=sin_half[:], in1=sin_half[:], op=ALU.mult)
-            nc.vector.tensor_scalar(
-                out=cos_t[:], in0=cos_t[:], scalar1=-2.0, scalar2=1.0, op0=ALU.mult, op1=ALU.add
-            )
-
-            def product(name, a, b):
-                result = table(name)
-                nc.vector.tensor_tensor(out=result[:], in0=a, in1=b, op=ALU.mult)
-                return result
-
-            coef = {"real": table("coef_real"), "imag": table("coef_imag")}
-            re_cos = product("re_cos", c_re, cos_t[:])
-            im_sin = product("im_sin", c_im, sin_t[:])
-            nc.vector.tensor_tensor(
-                out=coef["real"][:], in0=re_cos[:], in1=im_sin[:], op=ALU.subtract
-            )
-            re_sin = product("re_sin", c_re, sin_t[:])
-            im_cos = product("im_cos", c_im, cos_t[:])
-            nc.vector.scalar_tensor_tensor(
-                out=coef["imag"][:], in0=re_sin[:], scalar=-1.0, in1=im_cos[:],
-                op0=ALU.mult, op1=ALU.subtract,
-            )
-            re_re = product("re_re", c_re, b_re)
-            im_im = product("im_im", c_im, b_im)
-            nc.vector.tensor_tensor(out=re_re[:], in0=re_re[:], in1=im_im[:], op=ALU.subtract)
-            gain = keep.tile([P, TILES], F32, name="gain")
-            nc.vector.tensor_reduce(
-                out=gain[:], in_=re_re[:].rearrange("p (c s) -> p c s", s=S), axis=AXIS.X,
-                op=ALU.add,
-            )
-            for t in range(L_TILES):
-                for g in range(2):
-                    nc.vector.quantize_mx(
-                        out=h_codes[:, g, t * P : (t + 1) * P].bitcast(FP8X4),
-                        scales=h_scales[:, g, t * P : (t + 1) * P],
-                        in_=grouped_hs[t][:, g].rearrange("p l k -> p (l k)"),
+                for g in range(IN_PASSES):
+                    quantise_later(
+                        -QUANTISE_LAG,
+                        grouped_h[:, g].rearrange("p l k -> p (l k)"),
+                        h_codes[:, g, t * P : (t + 1) * P],
+                        h_scales[:, g, t * P : (t + 1) * P],
                     )
-            for c in range(D // K_PASS):
-                turn_weight_pass(c - QUANTISE_LAG, w_raws[0][:], c, w1_codes, w1_scales, 0)
 
-            y_sums = {}
+            re_sin = product(nc.gpsimd, "re_sin", c_re, minus_sin[:])
+            im_cos = product(nc.gpsimd, "im_cos", c_im, cos_t[:])
+            nc.gpsimd.tensor_tensor(
+                out=coef["imag"][:], in0=re_sin[:], in1=im_cos[:], op=ALU.subtract
+            )
+            re_re = product(nc.gpsimd, "re_re", c_re, b_re)
+            im_im = product(nc.gpsimd, "im_im", c_im, b_im)
+            nc.gpsimd.tensor_tensor(out=re_re[:], in0=re_re[:], in1=im_im[:], op=ALU.subtract)
+            by_state = re_re[:].rearrange("p (c s) -> p c s", s=S)
+            for width in (S // 2, S // 4):
+                nc.gpsimd.tensor_tensor(
+                    out=by_state[:, :, 0:width], in0=by_state[:, :, 0:width],
+                    in1=by_state[:, :, width : 2 * width], op=ALU.add,
+                )
+            gain = keep.tile([P, TILES], F32, name="gain")
+            nc.gpsimd.tensor_tensor(
+                out=gain[:], in0=by_state[:, :, 0], in1=by_state[:, :, 1], op=ALU.add
+            )
+
             slow_sums = {}
             w_out_raws = {}
 
@@ -309,7 +348,7 @@ def tile_recursivemamba130m_pa_kernel(
                 x_in = psum.tile([P, BANK], F32, tag="for_scalar")
                 cols = slice(256 * q + P * e, 256 * q + P * (e + 1))
                 for rows in (slice(0, 256), slice(256, L)):
-                    for c in range(D // K_PASS):
+                    for c in range(IN_PASSES):
                         nc.tensor.matmul_mx(
                             out=x_in[:, rows],
                             lhsT=w1_codes[:, c, cols].bitcast(FP8X4),
@@ -317,7 +356,7 @@ def tile_recursivemamba130m_pa_kernel(
                             rhs=h_codes[:, c, rows].bitcast(FP8X4),
                             rhs_scale=h_scales[:, c, rows],
                             start=(c == 0),
-                            stop=(c == D // K_PASS - 1),
+                            stop=(c == IN_PASSES - 1),
                         )
                 nc.scalar.activation(
                     out=term[:, e, :], in_=x_in[:, 0:L], func=ACT.Copy,
@@ -335,36 +374,23 @@ def tile_recursivemamba130m_pa_kernel(
                         scale=coefficient(which, q, e, w, 0),
                     )
 
-            def add_fast_word(q, j, turned):
+            def add_fast_state(q, j, h, turned):
                 g, u = divmod(q, 2)
                 which, w = FAST_WORDS[j]
-                for h in (1,) if j == 0 else (0, 1):
-                    for e in (1, 0):
-                        y_tile = y_sums[g][:, 2 * u + e, :]
-                        nc.vector.scalar_tensor_tensor(
-                            out=y_tile, in0=turned[e][:, 0:L, h],
-                            scalar=coefficient(which, q, e, w, h), in1=y_tile,
-                            op0=ALU.mult, op1=ALU.add,
-                        )
-
-            def round_pass(step, g):
-                for t in range(L_TILES):
-                    grouped_y = stage.tile([P, P, 4], BF16, tag="grouped_y", align_bytes=64)
-                    nc.scalar.copy(
-                        out=grouped_y[:],
-                        in_=y_sums[g][:, :, t * P : (t + 1) * P].rearrange("p k l -> p l k"),
+                for e in (1, 0):
+                    y_tile = y_sums[g][:, 2 * u + e, :]
+                    nc.vector.scalar_tensor_tensor(
+                        out=y_tile, in0=turned[e][:, 0:L, h],
+                        scalar=coefficient(which, q, e, w, h), in1=y_tile,
+                        op0=ALU.mult, op1=ALU.add,
                     )
-                    waiting[step] = waiting.get(step, []) + [
-                        (
-                            grouped_y[:].rearrange("p l k -> p (l k)"),
-                            y_codes[:, g, t * P : (t + 1) * P],
-                            y_scales[:, g, t * P : (t + 1) * P],
-                        )
-                    ]
 
             steps = [(q, j) for q in range(PAIRS) for j in range(STEPS)]
             turned_next = turn_word(0, FAST_WORDS[0][0], FAST_WORDS[0][1], "for_vector")
             start_sums(0, turned_next)
+            for c in range(IN_PASSES):
+                turn_weight_pass(-1, w_raws[0][:], c, w1_codes, w1_scales, 0)
+
             for step, (q, j) in enumerate(steps):
                 g, u = divmod(q, 2)
                 if j == 0:
@@ -375,7 +401,14 @@ def tile_recursivemamba130m_pa_kernel(
                         nc.sync.dma_start(out=w_out_raws[g][:], in_=w_out_blocks[g])
                     if q + 1 < PAIRS:
                         w_raws[q + 1] = load_w_in(q + 1)
-                        states[q + 1] = load_state(q + 1)
+                        load_state(q + 1, "real")
+                        load_state(q + 1, "imag")
+                    cols = slice(q * (D // PAIRS), (q + 1) * (D // PAIRS))
+                    nc.gpsimd.tensor_tensor(
+                        out=h_f32[:, :, cols], in0=x_sb[:, :, cols],
+                        in1=emb_rows[:, cols].unsqueeze(1).to_broadcast([P, L_TILES, D // PAIRS]),
+                        op=ALU.add,
+                    )
 
                 turned = turned_next
                 if step + 1 < len(steps):
@@ -392,103 +425,124 @@ def tile_recursivemamba130m_pa_kernel(
                     e = j - 2
                     if e == 0:
                         x_term = products.tile([P, 2, L], F32, tag="term")
-                        if u == 0 and g > 0:
-                            round_pass(step, g - 1)
                     project_in(q, e, x_term)
                     if e == 1:
                         nc.gpsimd.tensor_tensor(
                             out=slow_sums[q][:], in0=slow_sums[q][:], in1=x_term[:], op=ALU.add
                         )
-                else:
-                    c = j - 4
                     if q + 1 < PAIRS:
                         turn_weight_pass(
-                            step, w_raws[q + 1][:], c, w1_codes, w1_scales, 256 * (q + 1)
+                            step, w_raws[q + 1][:], e, w1_codes, w1_scales, 256 * (q + 1)
                         )
+                    else:
+                        turn_weight_pass(
+                            step, w_out_raws[g][:], 2 * u + e, w2_codes, w2_scales, 256 * g
+                        )
+                    if e == 1 and u == 0 and g > 0:
+                        for t in range(L_TILES):
+                            round_block(step, g - 1, t)
+                elif q + 1 < PAIRS:
                     turn_weight_pass(
-                        step, w_out_raws[g][:], 2 * u + c, w2_codes, w2_scales, 256 * g
+                        step, w_out_raws[g][:], 2 * u + j - 4, w2_codes, w2_scales, 256 * g
                     )
 
-                quantise_waiting(step - QUANTISE_LAG)
-                add_fast_word(q, j, turned)
+                if j == 0 or step < QUANTISE_LAG:
+                    quantise_waiting(step - QUANTISE_LAG)
+                for h in (1,) if j == 0 else (0, 1):
+                    add_fast_state(q, j, h, turned)
                 if j == STEPS - 1:
-                    for t in range(L_TILES):
-                        rows = slice(t * P, (t + 1) * P)
+                    blocks = L_TILES if u == 1 else 1
+                    for t in range(blocks):
+                        rows = slice(t * (L // blocks), (t + 1) * (L // blocks))
                         y_block = y_sums[g][:, 2 * u : 2 * u + 2, rows]
                         nc.gpsimd.tensor_tensor(
                             out=y_block, in0=y_block, in1=slow_sums[q][:, :, rows], op=ALU.add
                         )
 
-            for step in range(len(steps), len(steps) + QUANTISE_LAG):
-                quantise_waiting(step - QUANTISE_LAG)
-            early_root = keep.tile([P, 1], F32, name="early_root")
-            nc.scalar.activation(out=early_root[:], in_=eps_column[:], func=ACT.Sqrt)
-            round_pass(len(steps), F // K_PASS - 1)
-            quantise_waiting(len(steps))
+            quantise_waiting(len(steps) - QUANTISE_LAG)
             nc.sync.dma_start(out=mixer_rows[:], in_=mixer_norm_w.partition_broadcast(P))
             nc.sync.dma_start(out=loop_rows[:], in_=loop_norm_w.partition_broadcast(P))
+            early_root = keep.tile([P, 1], F32, name="early_root")
+            nc.scalar.activation(out=early_root[:], in_=eps_column[:], func=ACT.Sqrt)
+            for half in range(HALVES):
+                for t in range(L_TILES):
+                    ring = "for_scalar" if len(projections) < RING else "for_vector"
+                    projections[(t, half)] = psum.tile(
+                        [P, BANK], F32, tag=ring, name="projection"
+                    )
+                    project_out(t, half, range(OUT_PASSES - 1))
 
         with ExitStack() as ending:
-            tail = ending.enter_context(tc.tile_pool(name="tail", bufs=2))
-            psum_tail = ending.enter_context(tc.psum_pool(name="psum_tail", bufs=6))
+            tail = ending.enter_context(tc.tile_pool(name="tail", bufs=L_TILES))
             out_tiles = out.rearrange("b (t p) d -> (b t) p d", p=P)
-            halves = D // BANK
+            half_squares, mixed, proj_roots, residuals, res_roots, results = {}, {}, {}, {}, {}, {}
 
-            def inverse_rms(square_sum):
-                root = tail.tile([P, 1], F32, tag="root")
+            def root_of_mean(square_sum, tag):
+                root = tail.tile([P, 1], F32, tag=tag, name=tag)
                 nc.scalar.activation(
                     out=root[:], in_=square_sum, func=ACT.Sqrt, bias=eps_column[:, 0:1],
                     scale=1.0 / D,
                 )
-                inverse = tail.tile([P, 1], F32, tag="inverse")
-                nc.vector.reciprocal(out=inverse[:], in_=root[:])
-                return inverse
+                return root
 
-            for t in range(L_TILES):
-                rows = slice(t * P, (t + 1) * P)
-                half_squares = tail.tile([P, halves], F32, tag="half_squares")
-                mixed = tail.tile([P, D], F32, tag="mixed")
-                for half in range(halves):
-                    cols = slice(half * BANK, (half + 1) * BANK)
-                    proj = psum_tail.tile([P, BANK], F32, tag="proj")
-                    for g in range(F // K_PASS):
-                        nc.tensor.matmul_mx(
-                            out=proj[:],
-                            lhsT=y_codes[:, g, rows].bitcast(FP8X4),
-                            lhsT_scale=y_scales[:, g, rows],
-                            rhs=w2_codes[:, g, cols].bitcast(FP8X4),
-                            rhs_scale=w2_scales[:, g, cols],
-                            start=(g == 0),
-                            stop=(g == F // K_PASS - 1),
-                        )
+            def inverse(root, tag):
+                one_over = tail.tile([P, 1], F32, tag=tag, name=tag)
+                nc.vector.reciprocal(out=one_over[:], in_=root[:])
+                return one_over
+
+            def square_projection(t):
+                half_squares[t] = tail.tile([P, HALVES], F32, tag="half_squares", name="half_squares")
+                mixed[t] = tail.tile([P, D], F32, tag="mixed", name="mixed")
+                for half in range(HALVES):
+                    project_out(t, half, [OUT_PASSES - 1])
                     nc.scalar.activation(
-                        out=mixed[:, cols], in_=proj[:], func=ACT.Square,
-                        accum_out=half_squares[:, half : half + 1],
+                        out=mixed[t][:, half * BANK : (half + 1) * BANK],
+                        in_=projections[(t, half)][:], func=ACT.Square,
+                        accum_out=half_squares[t][:, half : half + 1],
                     )
+
+            def mix(t):
+                for half in range(HALVES):
+                    cols = slice(half * BANK, (half + 1) * BANK)
                     nc.vector.tensor_tensor(
-                        out=mixed[:, cols], in0=proj[:], in1=mixer_rows[:, cols], op=ALU.mult
+                        out=mixed[t][:, cols], in0=projections[(t, half)][:],
+                        in1=mixer_rows[:, cols], op=ALU.mult,
                     )
                 proj_squares = tail.tile([P, 1], F32, tag="proj_squares")
                 nc.vector.tensor_tensor(
-                    out=proj_squares[:], in0=half_squares[:, 0:1], in1=half_squares[:, 1:2],
+                    out=proj_squares[:], in0=half_squares[t][:, 0:1], in1=half_squares[t][:, 1:2],
                     op=ALU.add,
                 )
-                proj_scale = inverse_rms(proj_squares[:])
+                proj_roots[t] = root_of_mean(proj_squares[:], "proj_root")
 
-                residual = tail.tile([P, D], F32, tag="residual")
+            def add_residual(t):
+                proj_scale = inverse(proj_roots[t], "proj_scale")
+                residuals[t] = tail.tile([P, D], F32, tag="residual", name="residual")
                 nc.vector.scalar_tensor_tensor(
-                    out=residual[:], in0=mixed[:], scalar=proj_scale[:, 0:1], in1=h_f32[:, t, :],
-                    op0=ALU.mult, op1=ALU.add,
+                    out=residuals[t][:], in0=mixed[t][:], scalar=proj_scale[:, 0:1],
+                    in1=h_f32[:, t, :], op0=ALU.mult, op1=ALU.add,
                 )
                 squared = tail.tile([P, D], F32, tag="squared")
                 res_squares = tail.tile([P, 1], F32, tag="res_squares")
                 nc.scalar.activation(
-                    out=squared[:], in_=residual[:], func=ACT.Square, accum_out=res_squares[:]
+                    out=squared[:], in_=residuals[t][:], func=ACT.Square, accum_out=res_squares[:]
                 )
-                result = tail.tile([P, D], F32, tag="result")
-                nc.gpsimd.tensor_tensor(
-                    out=result[:], in0=residual[:], in1=loop_rows[:], op=ALU.mult
+                res_roots[t] = root_of_mean(res_squares[:], "res_root")
+
+            def finish(t):
+                res_scale = inverse(res_roots[t], "res_scale")
+                results[t] = tail.tile([P, D], F32, tag="result", name="result")
+                nc.vector.scalar_tensor_tensor(
+                    out=results[t][:], in0=residuals[t][:], scalar=res_scale[:, 0:1],
+                    in1=loop_rows[:], op0=ALU.mult, op1=ALU.mult,
                 )
-                res_scale = inverse_rms(res_squares[:])
-                nc.vector.tensor_scalar_mul(out=result[:], in0=result[:], scalar1=res_scale[:, 0:1])
-                nc.sync.dma_start(out=out_tiles[t], in_=result[:])
+                nc.sync.dma_start(out=out_tiles[t], in_=results[t][:])
+
+            for t in range(L_TILES):
+                round_block(len(steps), OUT_PASSES - 1, t)
+                quantise_waiting(len(steps))
+            stages = (square_projection, mix, add_residual, finish)
+            for i in range(L_TILES + len(stages) - 1):
+                for lag, stage_of_block in enumerate(stages):
+                    if 0 <= i - lag < L_TILES:
+                        stage_of_block(i - lag)

@@ -385,6 +385,15 @@ def tile_recursivemamba130m_pa_kernel(
                         op0=ALU.mult, op1=ALU.add,
                     )
 
+            def join_sums(q, blocks):
+                g, u = divmod(q, 2)
+                for t in range(blocks):
+                    rows = slice(t * (L // blocks), (t + 1) * (L // blocks))
+                    y_block = y_sums[g][:, 2 * u : 2 * u + 2, rows]
+                    nc.gpsimd.tensor_tensor(
+                        out=y_block, in0=y_block, in1=slow_sums[q][:, :, rows], op=ALU.add
+                    )
+
             steps = [(q, j) for q in range(PAIRS) for j in range(STEPS)]
             turned_next = turn_word(0, FAST_WORDS[0][0], FAST_WORDS[0][1], "for_vector")
             start_sums(0, turned_next)
@@ -450,14 +459,10 @@ def tile_recursivemamba130m_pa_kernel(
                     quantise_waiting(step - QUANTISE_LAG)
                 for h in (1,) if j == 0 else (0, 1):
                     add_fast_state(q, j, h, turned)
-                if j == STEPS - 1:
-                    blocks = L_TILES if u == 1 else 1
-                    for t in range(blocks):
-                        rows = slice(t * (L // blocks), (t + 1) * (L // blocks))
-                        y_block = y_sums[g][:, 2 * u : 2 * u + 2, rows]
-                        nc.gpsimd.tensor_tensor(
-                            out=y_block, in0=y_block, in1=slow_sums[q][:, :, rows], op=ALU.add
-                        )
+                if j == 0 and q > 0:
+                    join_sums(q - 1, 1)
+
+            join_sums(PAIRS - 1, L_TILES)
 
             quantise_waiting(len(steps) - QUANTISE_LAG)
             nc.sync.dma_start(out=mixer_rows[:], in_=mixer_norm_w.partition_broadcast(P))

@@ -33,6 +33,7 @@ ALL_WORDS = [(which, w) for which in ("real", "imag") for w in range(WORDS)]
 SLOW_WORDS = ALL_WORDS[:2]
 FAST_WORDS = ALL_WORDS[2:]
 STEPS = len(FAST_WORDS)
+EARLY_H = 4
 assert len(SLOW_WORDS) == 2 and STEPS == 6 and IN_PASSES == 2
 QUANTISE_LAG = 2
 
@@ -83,6 +84,8 @@ def tile_recursivemamba130m_pa_kernel(
         loop_rows = keep.tile([P, D], BF16, name="loop_rows")
         eps_column = keep.tile([P, 1], F32, name="eps_column")
         y_sums = {}
+        slow_sums = {}
+        steps = [(q, j) for q in range(PAIRS) for j in range(STEPS)]
         projections = {}
         waiting = {}
 
@@ -103,6 +106,31 @@ def tile_recursivemamba130m_pa_kernel(
             quantise_later(
                 step, grouped_y[:].rearrange("p l k -> p (l k)"), y_codes[:, g, rows],
                 y_scales[:, g, rows],
+            )
+
+        grouped_last = {}
+
+        def round_first_half(t):
+            rows = slice(t * P, (t + 1) * P)
+            grouped_last[t] = stage.tile(
+                [P, P, 4], BF16, tag="grouped_y", name="grouped_y", align_bytes=64
+            )
+            nc.scalar.copy(
+                out=grouped_last[t][:, :, 0:2],
+                in_=y_sums[OUT_PASSES - 1][:, 0:2, rows].rearrange("p k l -> p l k"),
+            )
+
+        def round_second_half(t):
+            rows = slice(t * P, (t + 1) * P)
+            nc.vector.tensor_tensor(
+                out=grouped_last[t][:, :, 2:4],
+                in0=y_sums[OUT_PASSES - 1][:, 2:4, rows].rearrange("p k l -> p l k"),
+                in1=slow_sums[PAIRS - 1][:, :, rows].rearrange("p k l -> p l k"),
+                op=ALU.add,
+            )
+            quantise_later(
+                len(steps), grouped_last[t][:].rearrange("p l k -> p (l k)"),
+                y_codes[:, OUT_PASSES - 1, rows], y_scales[:, OUT_PASSES - 1, rows],
             )
 
         def project_out(t, half, passes):
@@ -317,7 +345,6 @@ def tile_recursivemamba130m_pa_kernel(
                 out=gain[:], in0=by_state[:, :, 0], in1=by_state[:, :, 1], op=ALU.add
             )
 
-            slow_sums = {}
             w_out_raws = {}
 
             def coefficient(which, q, e, w, h):
@@ -385,16 +412,31 @@ def tile_recursivemamba130m_pa_kernel(
                         op0=ALU.mult, op1=ALU.add,
                     )
 
-            def join_sums(q, blocks):
+            def join_sums(q):
                 g, u = divmod(q, 2)
-                for t in range(blocks):
-                    rows = slice(t * (L // blocks), (t + 1) * (L // blocks))
-                    y_block = y_sums[g][:, 2 * u : 2 * u + 2, rows]
-                    nc.gpsimd.tensor_tensor(
-                        out=y_block, in0=y_block, in1=slow_sums[q][:, :, rows], op=ALU.add
-                    )
+                y_pair = y_sums[g][:, 2 * u : 2 * u + 2, :]
+                nc.gpsimd.tensor_tensor(
+                    out=y_pair, in0=y_pair, in1=slow_sums[q][:], op=ALU.add
+                )
 
-            steps = [(q, j) for q in range(PAIRS) for j in range(STEPS)]
+            def start_projections(t):
+                ring = "for_scalar" if t < RING // HALVES else "for_vector"
+                for half in range(HALVES):
+                    projections[(t, half)] = psum.tile(
+                        [P, BANK], F32, tag=ring, name="projection"
+                    )
+                    project_out(t, half, range(OUT_PASSES - 1 if half == 0 else 1))
+
+            def add_h(i):
+                cols = slice(i * (D // PAIRS), (i + 1) * (D // PAIRS))
+                nc.gpsimd.tensor_tensor(
+                    out=h_f32[:, :, cols], in0=x_sb[:, :, cols],
+                    in1=emb_rows[:, cols].unsqueeze(1).to_broadcast([P, L_TILES, D // PAIRS]),
+                    op=ALU.add,
+                )
+
+            for i in range(EARLY_H):
+                add_h(i)
             turned_next = turn_word(0, FAST_WORDS[0][0], FAST_WORDS[0][1], "for_vector")
             start_sums(0, turned_next)
             for c in range(IN_PASSES):
@@ -412,12 +454,8 @@ def tile_recursivemamba130m_pa_kernel(
                         w_raws[q + 1] = load_w_in(q + 1)
                         load_state(q + 1, "real")
                         load_state(q + 1, "imag")
-                    cols = slice(q * (D // PAIRS), (q + 1) * (D // PAIRS))
-                    nc.gpsimd.tensor_tensor(
-                        out=h_f32[:, :, cols], in0=x_sb[:, :, cols],
-                        in1=emb_rows[:, cols].unsqueeze(1).to_broadcast([P, L_TILES, D // PAIRS]),
-                        op=ALU.add,
-                    )
+                    if q + EARLY_H < PAIRS:
+                        add_h(q + EARLY_H)
 
                 turned = turned_next
                 if step + 1 < len(steps):
@@ -460,71 +498,74 @@ def tile_recursivemamba130m_pa_kernel(
                 for h in (1,) if j == 0 else (0, 1):
                     add_fast_state(q, j, h, turned)
                 if j == 0 and q > 0:
-                    join_sums(q - 1, 1)
+                    join_sums(q - 1)
+                if q == PAIRS - 1 and j == STEPS - 2:
+                    start_projections(0)
+                    for t in range(L_TILES):
+                        round_first_half(t)
+                if q == PAIRS - 1 and j == STEPS - 1:
+                    start_projections(1)
 
-            join_sums(PAIRS - 1, L_TILES)
-
-            quantise_waiting(len(steps) - QUANTISE_LAG)
+            round_second_half(0)
+            quantise_waiting(len(steps))
+            project_out(0, 1, range(1, OUT_PASSES - 1))
             nc.sync.dma_start(out=mixer_rows[:], in_=mixer_norm_w.partition_broadcast(P))
             nc.sync.dma_start(out=loop_rows[:], in_=loop_norm_w.partition_broadcast(P))
             early_root = keep.tile([P, 1], F32, name="early_root")
-            nc.scalar.activation(out=early_root[:], in_=eps_column[:], func=ACT.Sqrt)
-            for half in range(HALVES):
-                for t in range(L_TILES):
-                    ring = "for_scalar" if len(projections) < RING else "for_vector"
-                    projections[(t, half)] = psum.tile(
-                        [P, BANK], F32, tag=ring, name="projection"
-                    )
-                    project_out(t, half, range(OUT_PASSES - 1))
-
+            nc.scalar.activation(out=early_root[:], in_=eps_column[:], func=ACT.Abs_reciprocal_sqrt)
         with ExitStack() as ending:
             tail = ending.enter_context(tc.tile_pool(name="tail", bufs=L_TILES))
             out_tiles = out.rearrange("b (t p) d -> (b t) p d", p=P)
-            half_squares, mixed, proj_roots, residuals, res_roots, results = {}, {}, {}, {}, {}, {}
+            half_squares, mixed, proj_scales, residuals, res_scales, results = {}, {}, {}, {}, {}, {}
 
-            def root_of_mean(square_sum, tag):
-                root = tail.tile([P, 1], F32, tag=tag, name=tag)
+            def inverse_root(square_sum, bias, tag):
+                result = tail.tile([P, 1], F32, tag=tag, name=tag)
                 nc.scalar.activation(
-                    out=root[:], in_=square_sum, func=ACT.Sqrt, bias=eps_column[:, 0:1],
+                    out=result[:], in_=square_sum, func=ACT.Abs_reciprocal_sqrt, bias=bias,
                     scale=1.0 / D,
                 )
-                return root
+                return result
 
-            def inverse(root, tag):
-                one_over = tail.tile([P, 1], F32, tag=tag, name=tag)
-                nc.vector.reciprocal(out=one_over[:], in_=root[:])
-                return one_over
+            def square(t, half, squares):
+                nc.scalar.activation(
+                    out=squares[:, half * BANK : (half + 1) * BANK],
+                    in_=projections[(t, half)][:], func=ACT.Square,
+                    accum_out=half_squares[t][:, half : half + 1],
+                )
 
-            def square_projection(t):
+            def mix(t, half):
+                cols = slice(half * BANK, (half + 1) * BANK)
+                nc.vector.tensor_tensor(
+                    out=mixed[t][:, cols], in0=projections[(t, half)][:], in1=mixer_rows[:, cols],
+                    op=ALU.mult,
+                )
+
+            def square_and_mix(t):
                 half_squares[t] = tail.tile([P, HALVES], F32, tag="half_squares", name="half_squares")
                 mixed[t] = tail.tile([P, D], F32, tag="mixed", name="mixed")
                 for half in range(HALVES):
                     project_out(t, half, [OUT_PASSES - 1])
-                    nc.scalar.activation(
-                        out=mixed[t][:, half * BANK : (half + 1) * BANK],
-                        in_=projections[(t, half)][:], func=ACT.Square,
-                        accum_out=half_squares[t][:, half : half + 1],
-                    )
-
-            def mix(t):
+                squares = tail.tile([P, D], F32, tag="squared", name="squared")
                 for half in range(HALVES):
-                    cols = slice(half * BANK, (half + 1) * BANK)
-                    nc.vector.tensor_tensor(
-                        out=mixed[t][:, cols], in0=projections[(t, half)][:],
-                        in1=mixer_rows[:, cols], op=ALU.mult,
-                    )
-                proj_squares = tail.tile([P, 1], F32, tag="proj_squares")
-                nc.vector.tensor_tensor(
-                    out=proj_squares[:], in0=half_squares[t][:, 0:1], in1=half_squares[t][:, 1:2],
-                    op=ALU.add,
+                    if t == 0:
+                        square(t, half, squares)
+                        mix(t, HALVES - 1 - half)
+                    else:
+                        mix(t, half)
+                        square(t, half, squares)
+                half_mean = tail.tile([P, 1], F32, tag="half_mean")
+                nc.scalar.activation(
+                    out=half_mean[:], in_=half_squares[t][:, 0:1], func=ACT.Identity,
+                    bias=eps_column[:, 0:1], scale=1.0 / D,
                 )
-                proj_roots[t] = root_of_mean(proj_squares[:], "proj_root")
+                proj_scales[t] = inverse_root(
+                    half_squares[t][:, 1:2], half_mean[:, 0:1], "proj_scale"
+                )
 
             def add_residual(t):
-                proj_scale = inverse(proj_roots[t], "proj_scale")
                 residuals[t] = tail.tile([P, D], F32, tag="residual", name="residual")
                 nc.vector.scalar_tensor_tensor(
-                    out=residuals[t][:], in0=mixed[t][:], scalar=proj_scale[:, 0:1],
+                    out=residuals[t][:], in0=mixed[t][:], scalar=proj_scales[t][:, 0:1],
                     in1=h_f32[:, t, :], op0=ALU.mult, op1=ALU.add,
                 )
                 squared = tail.tile([P, D], F32, tag="squared")
@@ -532,22 +573,32 @@ def tile_recursivemamba130m_pa_kernel(
                 nc.scalar.activation(
                     out=squared[:], in_=residuals[t][:], func=ACT.Square, accum_out=res_squares[:]
                 )
-                res_roots[t] = root_of_mean(res_squares[:], "res_root")
+                res_scales[t] = inverse_root(res_squares[:], eps_column[:, 0:1], "res_scale")
 
             def finish(t):
-                res_scale = inverse(res_roots[t], "res_scale")
                 results[t] = tail.tile([P, D], F32, tag="result", name="result")
-                nc.vector.scalar_tensor_tensor(
-                    out=results[t][:], in0=residuals[t][:], scalar=res_scale[:, 0:1],
-                    in1=loop_rows[:], op0=ALU.mult, op1=ALU.mult,
-                )
-                nc.sync.dma_start(out=out_tiles[t], in_=results[t][:])
+                parts = HALVES if t == L_TILES - 1 else 1
+                for part in range(parts):
+                    cols = slice(part * (D // parts), (part + 1) * (D // parts))
+                    nc.vector.scalar_tensor_tensor(
+                        out=results[t][:, cols], in0=residuals[t][:, cols],
+                        scalar=res_scales[t][:, 0:1], in1=loop_rows[:, cols],
+                        op0=ALU.mult, op1=ALU.mult,
+                    )
+                    nc.sync.dma_start(out=out_tiles[t][:, cols], in_=results[t][:, cols])
 
-            for t in range(L_TILES):
-                round_block(len(steps), OUT_PASSES - 1, t)
-                quantise_waiting(len(steps))
-            stages = (square_projection, mix, add_residual, finish)
-            for i in range(L_TILES + len(stages) - 1):
-                for lag, stage_of_block in enumerate(stages):
-                    if 0 <= i - lag < L_TILES:
-                        stage_of_block(i - lag)
+            for t in range(1, L_TILES):
+                round_second_half(t)
+            quantise_waiting(len(steps))
+            square_and_mix(0)
+            project_out(1, 1, range(1, OUT_PASSES - 1))
+            square_and_mix(1)
+            start_projections(2)
+            project_out(2, 1, range(1, OUT_PASSES - 1))
+            add_residual(0)
+            square_and_mix(2)
+            add_residual(1)
+            finish(0)
+            add_residual(2)
+            finish(1)
+            finish(2)

@@ -72,8 +72,8 @@ def tile_recursivemamba130m_pa_kernel(
 
         h_codes = keep.tile([P, IN_PASSES, L], U32, name="h_codes", align_bytes=64)
         h_scales = keep.tile([P, IN_PASSES, L], U8, name="h_scales", align_bytes=64)
-        w1_codes = keep.tile([P, IN_PASSES, F], U32, name="w1_codes", align_bytes=64)
-        w1_scales = keep.tile([P, IN_PASSES, F], U8, name="w1_scales", align_bytes=64)
+        w1_codes = keep.tile([P, PAIRS, IN_PASSES, 256], U32, name="w1_codes", align_bytes=64)
+        w1_scales = keep.tile([P, PAIRS, IN_PASSES, 256], U8, name="w1_scales", align_bytes=64)
         y_codes = keep.tile([P, OUT_PASSES, L], U32, name="y_codes", align_bytes=64)
         y_scales = keep.tile([P, OUT_PASSES, L], U8, name="y_scales", align_bytes=64)
         w2_codes = keep.tile([P, OUT_PASSES, D], U32, name="w2_codes", align_bytes=64)
@@ -99,21 +99,25 @@ def tile_recursivemamba130m_pa_kernel(
                         nc.vector.quantize_mx(out=codes.bitcast(FP8X4), scales=scales, in_=grouped)
                     waiting[step] = []
 
-        def round_block(step, g, t):
-            rows = slice(t * P, (t + 1) * P)
-            grouped_y = stage.tile([P, P, 4], BF16, tag="grouped_y", align_bytes=64)
-            nc.scalar.copy(out=grouped_y[:], in_=y_sums[g][:, :, rows].rearrange("p k l -> p l k"))
-            quantise_later(
-                step, grouped_y[:].rearrange("p l k -> p (l k)"), y_codes[:, g, rows],
-                y_scales[:, g, rows],
-            )
+        def round_pass(step, g):
+            for rows in (slice(0, 256), slice(256, L)):
+                count = rows.stop - rows.start
+                grouped_y = stage.tile([P, 256, 4], BF16, tag="grouped_y", align_bytes=64)
+                nc.scalar.copy(
+                    out=grouped_y[:, 0:count, :],
+                    in_=y_sums[g][:, :, rows].rearrange("p k l -> p l k"),
+                )
+                quantise_later(
+                    step, grouped_y[:, 0:count, :].rearrange("p l k -> p (l k)"),
+                    y_codes[:, g, rows], y_scales[:, g, rows],
+                )
 
         grouped_last = {}
 
         def round_first_half(t):
             rows = slice(t * P, (t + 1) * P)
             grouped_last[t] = stage.tile(
-                [P, P, 4], BF16, tag="grouped_y", name="grouped_y", align_bytes=64
+                [P, P, 4], BF16, tag="grouped_last", name="grouped_last", align_bytes=64
             )
             nc.scalar.copy(
                 out=grouped_last[t][:, :, 0:2],
@@ -167,7 +171,7 @@ def tile_recursivemamba130m_pa_kernel(
                 "imag": imag.rearrange("b l c d s -> (b l) (c d s)"),
             }
             w_in_pairs = w_in.rearrange("(q p e) k -> q p e k", p=P, e=2)
-            w_out_blocks = out_proj_w.rearrange("(r i p) k -> r p i k", i=2, p=P)
+            w_out_blocks = out_proj_w.rearrange("(r i p) k -> r p i k", i=4, p=P)
             states = {}
 
             def load_table(table, name):
@@ -208,7 +212,7 @@ def tile_recursivemamba130m_pa_kernel(
             b_im = load_table(B_imag, "b_im")
             load_state(0, "imag")
 
-            def turn_weight_pass(step, raw, g, codes, scales, col0):
+            def turn_weight(raw, first_row, g, grouped):
                 raw_words = raw.bitcast(F32)
                 turned = psum.tile([P, BANK], F32, tag="for_scalar")
                 for u in range(2):
@@ -216,17 +220,42 @@ def tile_recursivemamba130m_pa_kernel(
                         first = 256 * g + 128 * u
                         nc.tensor.transpose(
                             turned[:, (2 * u + i) * P : (2 * u + i + 1) * P],
-                            raw_words[:, i, first : first + P],
+                            raw_words[:, first_row + i, first : first + P],
                             ident_f32[:],
                         )
-                grouped = stage.tile([P, 4 * 256], BF16, tag="grouped_w", bufs=6, align_bytes=64)
                 nc.scalar.copy(
-                    out=grouped[:].bitcast(F32).rearrange("p (r u) -> p r u", u=2),
+                    out=grouped.bitcast(F32).rearrange("p (r u) -> p r u", u=2),
                     in_=turned[:].rearrange("p (u r) -> p r u", u=2),
                 )
-                quantise_later(
-                    step, grouped[:], codes[:, g, col0 : col0 + 256], scales[:, g, col0 : col0 + 256]
-                )
+
+            def turn_w_in(step, q, c):
+                if c == 0:
+                    grouped_w_in[q] = stage.tile(
+                        [P, IN_PASSES, 4 * 256], BF16, tag="grouped_w_in", name="grouped_w_in",
+                        align_bytes=64,
+                    )
+                turn_weight(w_raws[q][:], 0, c, grouped_w_in[q][:, c, :])
+                if c == IN_PASSES - 1:
+                    quantise_later(
+                        step, grouped_w_in[q][:].rearrange("p c n -> p (c n)"),
+                        w1_codes[:, q].rearrange("p c n -> p (c n)"),
+                        w1_scales[:, q].rearrange("p c n -> p (c n)"),
+                    )
+
+            def turn_w_out(step, q, part):
+                half, g = divmod(q, OUT_PASSES)
+                if part == 0:
+                    grouped_w_out[q] = stage.tile(
+                        [P, 2, 4 * 256], BF16, tag="grouped_w_out", name="grouped_w_out",
+                        align_bytes=64,
+                    )
+                turn_weight(w_out_raws[q // 2][:], 2 * part, g % 2, grouped_w_out[q][:, part, :])
+                if part == 1:
+                    cols = slice(half * BANK, (half + 1) * BANK)
+                    quantise_later(
+                        step, grouped_w_out[q][:].rearrange("p i n -> p (i n)"),
+                        w2_codes[:, g, cols], w2_scales[:, g, cols],
+                    )
 
             def turn_word(q, which, w, ring):
                 views = []
@@ -345,7 +374,7 @@ def tile_recursivemamba130m_pa_kernel(
                 out=gain[:], in0=by_state[:, :, 0], in1=by_state[:, :, 1], op=ALU.add
             )
 
-            w_out_raws = {}
+            w_out_raws, grouped_w_in, grouped_w_out = {}, {}, {}
 
             def coefficient(which, q, e, w, h):
                 column = (2 * q + e) * S + 2 * w + h
@@ -371,24 +400,31 @@ def tile_recursivemamba130m_pa_kernel(
                             out=slow_sums[q][:], in0=slow_sums[q][:], in1=term[:], op=ALU.add
                         )
 
-            def project_in(q, e, term):
+            def project_in(q, e):
                 x_in = psum.tile([P, BANK], F32, tag="for_scalar")
-                cols = slice(256 * q + P * e, 256 * q + P * (e + 1))
+                cols = slice(P * e, P * (e + 1))
                 for rows in (slice(0, 256), slice(256, L)):
                     for c in range(IN_PASSES):
                         nc.tensor.matmul_mx(
                             out=x_in[:, rows],
-                            lhsT=w1_codes[:, c, cols].bitcast(FP8X4),
-                            lhsT_scale=w1_scales[:, c, cols],
+                            lhsT=w1_codes[:, q, c, cols].bitcast(FP8X4),
+                            lhsT_scale=w1_scales[:, q, c, cols],
                             rhs=h_codes[:, c, rows].bitcast(FP8X4),
                             rhs_scale=h_scales[:, c, rows],
                             start=(c == 0),
                             stop=(c == IN_PASSES - 1),
                         )
-                nc.scalar.activation(
-                    out=term[:, e, :], in_=x_in[:, 0:L], func=ACT.Copy,
-                    scale=gain[:, 2 * q + e : 2 * q + e + 1],
-                )
+                return x_in
+
+            def add_x_in(q, x_ins):
+                g, u = divmod(q, 2)
+                for e in (1, 0):
+                    y_tile = y_sums[g][:, 2 * u + e, :]
+                    nc.vector.scalar_tensor_tensor(
+                        out=y_tile, in0=x_ins[e][:, 0:L],
+                        scalar=gain[:, 2 * q + e : 2 * q + e + 1], in1=y_tile,
+                        op0=ALU.mult, op1=ALU.add,
+                    )
 
             def start_sums(q, turned):
                 g, u = divmod(q, 2)
@@ -425,7 +461,7 @@ def tile_recursivemamba130m_pa_kernel(
                     projections[(t, half)] = psum.tile(
                         [P, BANK], F32, tag=ring, name="projection"
                     )
-                    project_out(t, half, range(OUT_PASSES - 1 if half == 0 else 1))
+                    project_out(t, half, range(OUT_PASSES - 1))
 
             def add_h(i):
                 cols = slice(i * (D // PAIRS), (i + 1) * (D // PAIRS))
@@ -440,16 +476,21 @@ def tile_recursivemamba130m_pa_kernel(
             turned_next = turn_word(0, FAST_WORDS[0][0], FAST_WORDS[0][1], "for_vector")
             start_sums(0, turned_next)
             for c in range(IN_PASSES):
-                turn_weight_pass(-1, w_raws[0][:], c, w1_codes, w1_scales, 0)
+                turn_w_in(-1, 0, c)
 
             for step, (q, j) in enumerate(steps):
                 g, u = divmod(q, 2)
                 if j == 0:
                     if u == 0:
                         w_out_raws[g] = weights.tile(
-                            [P, 2, F], BF16, tag="w_out_raw", name="w_out_raw"
+                            [P, 4, 2 * K_PASS], BF16, tag="w_out_raw", name="w_out_raw"
                         )
-                        nc.sync.dma_start(out=w_out_raws[g][:], in_=w_out_blocks[g])
+                        half, two_passes = divmod(g, HALVES)
+                        first = two_passes * 2 * K_PASS
+                        nc.sync.dma_start(
+                            out=w_out_raws[g][:],
+                            in_=w_out_blocks[half][:, :, first : first + 2 * K_PASS],
+                        )
                     if q + 1 < PAIRS:
                         w_raws[q + 1] = load_w_in(q + 1)
                         load_state(q + 1, "real")
@@ -458,6 +499,8 @@ def tile_recursivemamba130m_pa_kernel(
                         add_h(q + EARLY_H)
 
                 turned = turned_next
+                if j < 2:
+                    add_slow_word(q, j)
                 if step + 1 < len(steps):
                     next_q, next_j = steps[step + 1]
                     turned_next = turn_word(
@@ -466,37 +509,26 @@ def tile_recursivemamba130m_pa_kernel(
                     if next_j == 0:
                         start_sums(next_q, turned_next)
 
-                if j < 2:
-                    add_slow_word(q, j)
-                elif j < 4:
+                if j in (2, 3):
                     e = j - 2
                     if e == 0:
-                        x_term = products.tile([P, 2, L], F32, tag="term")
-                    project_in(q, e, x_term)
-                    if e == 1:
-                        nc.gpsimd.tensor_tensor(
-                            out=slow_sums[q][:], in0=slow_sums[q][:], in1=x_term[:], op=ALU.add
-                        )
+                        x_ins = [project_in(q, i) for i in range(2)]
                     if q + 1 < PAIRS:
-                        turn_weight_pass(
-                            step, w_raws[q + 1][:], e, w1_codes, w1_scales, 256 * (q + 1)
-                        )
+                        turn_w_in(step, q + 1, e)
                     else:
-                        turn_weight_pass(
-                            step, w_out_raws[g][:], 2 * u + e, w2_codes, w2_scales, 256 * g
-                        )
+                        turn_w_out(step, q, e)
                     if e == 1 and u == 0 and g > 0:
-                        for t in range(L_TILES):
-                            round_block(step, g - 1, t)
-                elif q + 1 < PAIRS:
-                    turn_weight_pass(
-                        step, w_out_raws[g][:], 2 * u + j - 4, w2_codes, w2_scales, 256 * g
-                    )
+                        round_pass(step, g - 1)
+                elif j == 4 and q + 1 < PAIRS:
+                    for part in range(2):
+                        turn_w_out(step, q, part)
 
                 if j == 0 or step < QUANTISE_LAG:
                     quantise_waiting(step - QUANTISE_LAG)
                 for h in (1,) if j == 0 else (0, 1):
                     add_fast_state(q, j, h, turned)
+                if j == 3:
+                    add_x_in(q, x_ins)
                 if j == 0 and q > 0:
                     join_sums(q - 1)
                 if q == PAIRS - 1 and j == STEPS - 2:
@@ -508,7 +540,6 @@ def tile_recursivemamba130m_pa_kernel(
 
             round_second_half(0)
             quantise_waiting(len(steps))
-            project_out(0, 1, range(1, OUT_PASSES - 1))
             nc.sync.dma_start(out=mixer_rows[:], in_=mixer_norm_w.partition_broadcast(P))
             nc.sync.dma_start(out=loop_rows[:], in_=loop_norm_w.partition_broadcast(P))
             early_root = keep.tile([P, 1], F32, name="early_root")
@@ -591,10 +622,8 @@ def tile_recursivemamba130m_pa_kernel(
                 round_second_half(t)
             quantise_waiting(len(steps))
             square_and_mix(0)
-            project_out(1, 1, range(1, OUT_PASSES - 1))
             square_and_mix(1)
             start_projections(2)
-            project_out(2, 1, range(1, OUT_PASSES - 1))
             add_residual(0)
             square_and_mix(2)
             add_residual(1)

from contextlib import ExitStack
import math

import concourse.mybir as mybir
from concourse.masks import make_identity

F32 = mybir.dt.float32
BF16 = mybir.dt.bfloat16
U32 = mybir.dt.uint32
U8 = mybir.dt.uint8
FP8X4 = mybir.dt.float8_e4m3fn_x4
ALU = mybir.AluOpType
ACT = mybir.ActivationFunctionType

P = 128
L = 384
D = 1024
F = 2048
S = 8
EPS = 1e-6

L_TILES = L // P
K_PASS = 512
IN_PASSES = D // K_PASS
OUT_PASSES = F // K_PASS
PAIRS = F // 256
TILES = 2 * PAIRS
WORDS = S // 2
BANK = 512
HALVES = D // BANK
RING = 4
ALL_WORDS = [(which, w) for which in ("real", "imag") for w in range(WORDS)]
SLOW_WORDS = ALL_WORDS[:2]
FAST_WORDS = ALL_WORDS[2:]
STEPS = len(FAST_WORDS)
EARLY_H = 4
assert len(SLOW_WORDS) == 2 and STEPS == 6 and IN_PASSES == 2
QUANTISE_LAG = 2

ROUND_MAGIC = 12582912.0
TWO_PI_HIGH = 6.28125
TWO_PI_LOW = 2.0 * math.pi - TWO_PI_HIGH
PI_BELOW = 3.1415925

FLOPS = 2 * L * D * F + 2 * L * F * D + 2 * 2 * S * L * F


def tile_recursivemamba130m_pa_kernel(
    tc,
    x,
    step_emb,
    w_in,
    real,
    imag,
    A_theta,
    B_real,
    B_imag,
    C_real,
    C_imag,
    out_proj_w,
    mixer_norm_w,
    loop_norm_w,
    out,
):
    nc = tc.nc
    with ExitStack() as whole:
        keep = whole.enter_context(tc.tile_pool(name="keep", bufs=1))
        psum = whole.enter_context(tc.psum_pool(name="psum", bufs=RING))
        stage = whole.enter_context(tc.tile_pool(name="stage", bufs=3))
        sums = whole.enter_context(tc.tile_pool(name="sums", bufs=2))
        whole.enter_context(tc.manual_schedule())

        h_codes = keep.tile([P, IN_PASSES, L], U32, name="h_codes", align_bytes=64)
        h_scales = keep.tile([P, IN_PASSES, L], U8, name="h_scales", align_bytes=64)
        w1_codes = keep.tile([P, PAIRS, IN_PASSES, 256], U32, name="w1_codes", align_bytes=64)
        w1_scales = keep.tile([P, PAIRS, IN_PASSES, 256], U8, name="w1_scales", align_bytes=64)
        y_codes = keep.tile([P, OUT_PASSES, L], U32, name="y_codes", align_bytes=64)
        y_scales = keep.tile([P, OUT_PASSES, L], U8, name="y_scales", align_bytes=64)
        w2_codes = keep.tile([P, OUT_PASSES, D], U32, name="w2_codes", align_bytes=64)
        w2_scales = keep.tile([P, OUT_PASSES, D], U8, name="w2_scales", align_bytes=64)
        h_f32 = keep.tile([P, L_TILES, D], F32, name="h_f32")
        emb_rows = keep.tile([P, D], BF16, name="emb_rows")
        mixer_rows = keep.tile([P, D], BF16, name="mixer_rows")
        loop_rows = keep.tile([P, D], BF16, name="loop_rows")
        eps_column = keep.tile([P, 1], F32, name="eps_column")
        y_sums = {}
        slow_sums = {}
        steps = [(q, j) for q in range(PAIRS) for j in range(STEPS)]
        projections = {}
        waiting = {}

        def quantise_later(step, grouped, codes, scales):
            waiting[step] = waiting.get(step, []) + [(grouped, codes, scales)]

        def quantise_waiting(last_step):
            for step in sorted(waiting):
                if step <= last_step:
                    for grouped, codes, scales in waiting[step]:
                        nc.vector.quantize_mx(out=codes.bitcast(FP8X4), scales=scales, in_=grouped)
                    waiting[step] = []

        def round_pass(step, g):
            for rows in (slice(0, 256), slice(256, L)):
                count = rows.stop - rows.start
                grouped_y = stage.tile([P, 256, 4], BF16, tag="grouped_y", align_bytes=64)
                nc.scalar.copy(
                    out=grouped_y[:, 0:count, :],
                    in_=y_sums[g][:, :, rows].rearrange("p k l -> p l k"),
                )
                quantise_later(
                    step, grouped_y[:, 0:count, :].rearrange("p l k -> p (l k)"),
                    y_codes[:, g, rows], y_scales[:, g, rows],
                )

        grouped_last = {}

        def round_first_half(t):
            rows = slice(t * P, (t + 1) * P)
            grouped_last[t] = stage.tile(
                [P, P, 4], BF16, tag="grouped_last", name="grouped_last", align_bytes=64
            )
            nc.scalar.copy(
                out=grouped_last[t][:, :, 0:2],
                in_=y_sums[OUT_PASSES - 1][:, 0:2, rows].rearrange("p k l -> p l k"),
            )

        def round_second_half(t):
            rows = slice(t * P, (t + 1) * P)
            nc.vector.tensor_tensor(
                out=grouped_last[t][:, :, 2:4],
                in0=y_sums[OUT_PASSES - 1][:, 2:4, rows].rearrange("p k l -> p l k"),
                in1=slow_sums[PAIRS - 1][:, :, rows].rearrange("p k l -> p l k"),
                op=ALU.add,
            )
            quantise_later(
                len(steps), grouped_last[t][:].rearrange("p l k -> p (l k)"),
                y_codes[:, OUT_PASSES - 1, rows], y_scales[:, OUT_PASSES - 1, rows],
            )

        def project_out(t, half, passes):
            rows = slice(t * P, (t + 1) * P)
            cols = slice(half * BANK, (half + 1) * BANK)
            for g in passes:
                nc.tensor.matmul_mx(
                    out=projections[(t, half)][:],
                    lhsT=y_codes[:, g, rows].bitcast(FP8X4),
                    lhsT_scale=y_scales[:, g, rows],
                    rhs=w2_codes[:, g, cols].bitcast(FP8X4),
                    rhs_scale=w2_scales[:, g, cols],
                    start=(g == 0),
                    stop=(g == OUT_PASSES - 1),
                )

        with ExitStack() as body:
            stream = body.enter_context(tc.tile_pool(name="stream", bufs=12))
            weights = body.enter_context(tc.tile_pool(name="weights", bufs=2))
            products = body.enter_context(tc.tile_pool(name="products", bufs=4))

            nc.vector.memset(eps_column[:], EPS)
            emb_alone = keep.tile([P, D], BF16, name="emb_alone")
            nc.vector.memset(emb_alone[:], 0.0)
            ones = keep.tile([P, P], BF16, name="ones")
            nc.vector.memset(ones[:], 1.0)
            ident_f32 = keep.tile([P, P], F32, name="ident_f32")
            make_identity(nc, ident_f32[:])
            ident_bf16 = keep.tile([P, P], BF16, name="ident_bf16")
            make_identity(nc, ident_bf16[:])

            state_rows = {
                "real": real.rearrange("b l c d s -> (b l) (c d s)"),
                "imag": imag.rearrange("b l c d s -> (b l) (c d s)"),
            }
            w_in_pairs = w_in.rearrange("(q p e) k -> q p e k", p=P, e=2)
            w_out_blocks = out_proj_w.rearrange("(r i p) k -> r p i k", i=4, p=P)
            states = {}

            def load_table(table, name):
                raw = keep.tile([P, PAIRS, 2 * S], BF16, name=name)
                nc.sync.dma_start(
                    out=raw[:],
                    in_=table.rearrange("c d s -> (c d) s").rearrange(
                        "(q p e) s -> p q (e s)", p=P, e=2
                    ),
                )
                return raw[:].rearrange("p q f -> p (q f)")

            def load_w_in(q):
                w_raw = weights.tile([P, 2, D], BF16, tag="w_raw")
                nc.sync.dma_start(out=w_raw[:], in_=w_in_pairs[q])
                return w_raw

            def load_state(q, which):
                for t in range(L_TILES):
                    chunk = stream.tile([P, 256 * S], BF16, tag="chunk")
                    nc.sync.dma_start(
                        out=chunk[:],
                        in_=state_rows[which][
                            t * P : (t + 1) * P, q * 256 * S : (q + 1) * 256 * S
                        ],
                    )
                    states[(q, which, t)] = chunk

            nc.sync.dma_start(out=emb_alone[0:1, :], in_=step_emb.rearrange("(o d) -> o d", o=1))
            x_sb = keep.tile([P, L_TILES, D], BF16, name="x_sb")
            nc.sync.dma_start(out=x_sb[:], in_=x.rearrange("b (t p) d -> p (b t) d", p=P))
            theta = load_table(A_theta, "theta")
            c_re = load_table(C_real, "c_re")
            c_im = load_table(C_imag, "c_im")
            load_state(0, "real")
            w_raws = {0: load_w_in(0)}
            b_re = load_table(B_real, "b_re")
            b_im = load_table(B_imag, "b_im")
            load_state(0, "imag")

            def turn_weight(raw, first_row, g, grouped):
                raw_words = raw.bitcast(F32)
                turned = psum.tile([P, BANK], F32, tag="for_scalar")
                for u in range(2):
                    for i in range(2):
                        first = 256 * g + 128 * u
                        nc.tensor.transpose(
                            turned[:, (2 * u + i) * P : (2 * u + i + 1) * P],
                            raw_words[:, first_row + i, first : first + P],
                            ident_f32[:],
                        )
                nc.scalar.copy(
                    out=grouped.bitcast(F32).rearrange("p (r u) -> p r u", u=2),
                    in_=turned[:].rearrange("p (u r) -> p r u", u=2),
                )

            def turn_w_in(step, q, c):
                if c == 0:
                    grouped_w_in[q] = stage.tile(
                        [P, IN_PASSES, 4 * 256], BF16, tag="grouped_w_in", name="grouped_w_in",
                        align_bytes=64,
                    )
                turn_weight(w_raws[q][:], 0, c, grouped_w_in[q][:, c, :])
                if c == IN_PASSES - 1:
                    quantise_later(
                        step, grouped_w_in[q][:].rearrange("p c n -> p (c n)"),
                        w1_codes[:, q].rearrange("p c n -> p (c n)"),
                        w1_scales[:, q].rearrange("p c n -> p (c n)"),
                    )

            def turn_w_out(step, q, part):
                half, g = divmod(q, OUT_PASSES)
                if part == 0:
                    grouped_w_out[q] = stage.tile(
                        [P, 2, 4 * 256], BF16, tag="grouped_w_out", name="grouped_w_out",
                        align_bytes=64,
                    )
                turn_weight(w_out_raws[q // 2][:], 2 * part, g % 2, grouped_w_out[q][:, part, :])
                if part == 1:
                    cols = slice(half * BANK, (half + 1) * BANK)
                    quantise_later(
                        step, grouped_w_out[q][:].rearrange("p i n -> p (i n)"),
                        w2_codes[:, g, cols], w2_scales[:, g, cols],
                    )

            def turn_word(q, which, w, ring):
                views = []
                for e in range(2):
                    bank = psum.tile([P, BANK], F32, tag=ring)
                    for t in range(L_TILES):
                        words = states[(q, which, t)][:].bitcast(F32).rearrange(
                            "l (p j) -> l p j", j=2 * WORDS
                        )
                        nc.tensor.transpose(
                            bank[:, t * P : (t + 1) * P], words[:, :, WORDS * e + w], ident_f32[:]
                        )
                    views.append(bank[:].bitcast(BF16).rearrange("p (l h) -> p l h", h=2))
                return views

            early_sine = keep.tile([P, 1], F32, name="early_sine")
            nc.scalar.activation(out=early_sine[:], in_=eps_column[:], func=ACT.Sin)

            for half in range(HALVES):
                cols = slice(half * BANK, (half + 1) * BANK)
                spread = psum.tile([P, BANK], F32, tag="for_scalar")
                nc.tensor.matmul(
                    out=spread[:], lhsT=ones[:], rhs=emb_alone[:, cols], start=True, stop=True
                )
                nc.scalar.copy(out=emb_rows[:, cols], in_=spread[:])

            h_bf16 = keep.tile([P, L_TILES, D], BF16, name="h_bf16")
            for t in range(L_TILES):
                nc.vector.tensor_tensor(
                    out=h_bf16[:, t, :], in0=x_sb[:, t, :], in1=emb_rows[:], op=ALU.add
                )

            def table(name):
                return keep.tile([P, TILES * S], F32, name=name)

            turns = table("turns")
            nc.vector.tensor_scalar(
                out=turns[:], in0=theta, scalar1=1.0 / (2.0 * math.pi), scalar2=ROUND_MAGIC,
                op0=ALU.mult, op1=ALU.add,
            )
            nc.vector.tensor_scalar_sub(out=turns[:], in0=turns[:], scalar1=ROUND_MAGIC)
            angle = table("angle")
            nc.vector.scalar_tensor_tensor(
                out=angle[:], in0=turns[:], scalar=-TWO_PI_HIGH, in1=theta,
                op0=ALU.mult, op1=ALU.add,
            )
            nc.vector.scalar_tensor_tensor(
                out=angle[:], in0=turns[:], scalar=-TWO_PI_LOW, in1=angle[:],
                op0=ALU.mult, op1=ALU.add,
            )
            nc.vector.tensor_scalar(
                out=angle[:], in0=angle[:], scalar1=-PI_BELOW, scalar2=PI_BELOW,
                op0=ALU.max, op1=ALU.min,
            )
            minus_sin = table("minus_sin")
            nc.scalar.activation(out=minus_sin[:], in_=angle[:], func=ACT.Sin, scale=-1.0)
            sin_half = table("sin_half")
            nc.scalar.activation(out=sin_half[:], in_=angle[:], func=ACT.Sin, scale=0.5)

            def product(engine, name, a, b):
                result = table(name)
                engine.tensor_tensor(out=result[:], in0=a, in1=b, op=ALU.mult)
                return result

            coef = {"real": table("coef_real"), "imag": table("coef_imag")}
            cos_t = product(nc.vector, "cos_t", sin_half[:], sin_half[:])
            im_sin = product(nc.vector, "im_sin", c_im, minus_sin[:])
            nc.vector.tensor_scalar(
                out=cos_t[:], in0=cos_t[:], scalar1=-2.0, scalar2=1.0, op0=ALU.mult, op1=ALU.add
            )
            re_cos = product(nc.vector, "re_cos", c_re, cos_t[:])
            nc.vector.tensor_tensor(
                out=coef["real"][:], in0=re_cos[:], in1=im_sin[:], op=ALU.add
            )

            for t in range(L_TILES):
                columns = h_bf16[:, t, :].rearrange("l (g u p e) -> l g u p e", g=2, u=2, e=2)
                turned_h = psum.tile([P, 2 * BANK], BF16, tag="for_scalar")
                for g in range(IN_PASSES):
                    for u in range(2):
                        for e in range(2):
                            slot = 4 * g + 2 * u + e
                            nc.tensor.transpose(
                                turned_h[:, slot * P : (slot + 1) * P],
                                columns[:, g, u, :, e],
                                ident_bf16[:],
                            )
                grouped_h = stage.tile([P, IN_PASSES, P, 4], BF16, tag="grouped_h", align_bytes=64)
                nc.scalar.copy(
                    out=grouped_h[:], in_=turned_h[:].rearrange("p (g k l) -> p g l k", g=2, k=4)
                )
                for g in range(IN_PASSES):
                    quantise_later(
                        -QUANTISE_LAG,
                        grouped_h[:, g].rearrange("p l k -> p (l k)"),
                        h_codes[:, g, t * P : (t + 1) * P],
                        h_scales[:, g, t * P : (t + 1) * P],
                    )

            re_sin = product(nc.gpsimd, "re_sin", c_re, minus_sin[:])
            im_cos = product(nc.gpsimd, "im_cos", c_im, cos_t[:])
            nc.gpsimd.tensor_tensor(
                out=coef["imag"][:], in0=re_sin[:], in1=im_cos[:], op=ALU.subtract
            )
            re_re = product(nc.gpsimd, "re_re", c_re, b_re)
            im_im = product(nc.gpsimd, "im_im", c_im, b_im)
            nc.gpsimd.tensor_tensor(out=re_re[:], in0=re_re[:], in1=im_im[:], op=ALU.subtract)
            by_state = re_re[:].rearrange("p (c s) -> p c s", s=S)
            for width in (S // 2, S // 4):
                nc.gpsimd.tensor_tensor(
                    out=by_state[:, :, 0:width], in0=by_state[:, :, 0:width],
                    in1=by_state[:, :, width : 2 * width], op=ALU.add,
                )
            gain = keep.tile([P, TILES], F32, name="gain")
            nc.gpsimd.tensor_tensor(
                out=gain[:], in0=by_state[:, :, 0], in1=by_state[:, :, 1], op=ALU.add
            )

            w_out_raws, grouped_w_in, grouped_w_out = {}, {}, {}

            def coefficient(which, q, e, w, h):
                column = (2 * q + e) * S + 2 * w + h
                return coef[which][:, column : column + 1]

            def add_slow_word(q, index):
                which, w = SLOW_WORDS[index]
                turned = turn_word(q, which, w, "for_scalar")
                for h in range(2):
                    first = index == 0 and h == 0
                    if first:
                        slow_sums[q] = sums.tile([P, 2, L], F32, tag="slow_sum", name="slow_sum")
                        term = slow_sums[q]
                    else:
                        term = products.tile([P, 2, L], F32, tag="term")
                    for e in range(2):
                        nc.scalar.activation(
                            out=term[:, e, :], in_=turned[e][:, 0:L, h], func=ACT.Copy,
                            scale=coefficient(which, q, e, w, h),
                        )
                    if not first:
                        nc.gpsimd.tensor_tensor(
                            out=slow_sums[q][:], in0=slow_sums[q][:], in1=term[:], op=ALU.add
                        )

            def project_in(q, e):
                x_in = psum.tile([P, BANK], F32, tag="for_scalar")
                cols = slice(P * e, P * (e + 1))
                for rows in (slice(0, 256), slice(256, L)):
                    for c in range(IN_PASSES):
                        nc.tensor.matmul_mx(
                            out=x_in[:, rows],
                            lhsT=w1_codes[:, q, c, cols].bitcast(FP8X4),
                            lhsT_scale=w1_scales[:, q, c, cols],
                            rhs=h_codes[:, c, rows].bitcast(FP8X4),
                            rhs_scale=h_scales[:, c, rows],
                            start=(c == 0),
                            stop=(c == IN_PASSES - 1),
                        )
                return x_in

            def add_x_in(q, x_ins):
                g, u = divmod(q, 2)
                for e in (1, 0):
                    y_tile = y_sums[g][:, 2 * u + e, :]
                    nc.vector.scalar_tensor_tensor(
                        out=y_tile, in0=x_ins[e][:, 0:L],
                        scalar=gain[:, 2 * q + e : 2 * q + e + 1], in1=y_tile,
                        op0=ALU.mult, op1=ALU.add,
                    )

            def start_sums(q, turned):
                g, u = divmod(q, 2)
                which, w = FAST_WORDS[0]
                if u == 0:
                    y_sums[g] = sums.tile([P, 4, L], F32, tag="y_sum", name="y_sum")
                for e in range(2):
                    nc.scalar.activation(
                        out=y_sums[g][:, 2 * u + e, :], in_=turned[e][:, 0:L, 0], func=ACT.Copy,
                        scale=coefficient(which, q, e, w, 0),
                    )

            def add_fast_state(q, j, h, turned):
                g, u = divmod(q, 2)
                which, w = FAST_WORDS[j]
                for e in (1, 0):
                    y_tile = y_sums[g][:, 2 * u + e, :]
                    nc.vector.scalar_tensor_tensor(
                        out=y_tile, in0=turned[e][:, 0:L, h],
                        scalar=coefficient(which, q, e, w, h), in1=y_tile,
                        op0=ALU.mult, op1=ALU.add,
                    )

            def join_sums(q):
                g, u = divmod(q, 2)
                y_pair = y_sums[g][:, 2 * u : 2 * u + 2, :]
                nc.gpsimd.tensor_tensor(
                    out=y_pair, in0=y_pair, in1=slow_sums[q][:], op=ALU.add
                )

            def start_projections(t):
                ring = "for_scalar" if t < RING // HALVES else "for_vector"
                for half in range(HALVES):
                    projections[(t, half)] = psum.tile(
                        [P, BANK], F32, tag=ring, name="projection"
                    )
                    project_out(t, half, range(OUT_PASSES - 1))

            def add_h(i):
                cols = slice(i * (D // PAIRS), (i + 1) * (D // PAIRS))
                nc.gpsimd.tensor_tensor(
                    out=h_f32[:, :, cols], in0=x_sb[:, :, cols],
                    in1=emb_rows[:, cols].unsqueeze(1).to_broadcast([P, L_TILES, D // PAIRS]),
                    op=ALU.add,
                )

            for i in range(EARLY_H):
                add_h(i)
            turned_next = turn_word(0, FAST_WORDS[0][0], FAST_WORDS[0][1], "for_vector")
            start_sums(0, turned_next)
            for c in range(IN_PASSES):
                turn_w_in(-1, 0, c)

            for step, (q, j) in enumerate(steps):
                g, u = divmod(q, 2)
                if j == 0:
                    if u == 0:
                        w_out_raws[g] = weights.tile(
                            [P, 4, 2 * K_PASS], BF16, tag="w_out_raw", name="w_out_raw"
                        )
                        half, two_passes = divmod(g, HALVES)
                        first = two_passes * 2 * K_PASS
                        nc.sync.dma_start(
                            out=w_out_raws[g][:],
                            in_=w_out_blocks[half][:, :, first : first + 2 * K_PASS],
                        )
                    if q + 1 < PAIRS:
                        w_raws[q + 1] = load_w_in(q + 1)
                        load_state(q + 1, "real")
                        load_state(q + 1, "imag")
                    if q + EARLY_H < PAIRS:
                        add_h(q + EARLY_H)

                turned = turned_next
                if j < 2:
                    add_slow_word(q, j)
                if step + 1 < len(steps):
                    next_q, next_j = steps[step + 1]
                    turned_next = turn_word(
                        next_q, FAST_WORDS[next_j][0], FAST_WORDS[next_j][1], "for_vector"
                    )
                    if next_j == 0:
                        start_sums(next_q, turned_next)

                if j in (2, 3):
                    e = j - 2
                    if e == 0:
                        x_ins = [project_in(q, i) for i in range(2)]
                    if q + 1 < PAIRS:
                        turn_w_in(step, q + 1, e)
                    else:
                        turn_w_out(step, q, e)
                    if e == 1 and u == 0 and g > 0:
                        round_pass(step, g - 1)
                elif j == 4 and q + 1 < PAIRS:
                    for part in range(2):
                        turn_w_out(step, q, part)

                if j == 0 or step < QUANTISE_LAG:
                    quantise_waiting(step - QUANTISE_LAG)
                for h in (1,) if j == 0 else (0, 1):
                    add_fast_state(q, j, h, turned)
                if j == 3:
                    add_x_in(q, x_ins)
                if j == 0 and q > 0:
                    join_sums(q - 1)
                if q == PAIRS - 1 and j == STEPS - 2:
                    start_projections(0)
                    for t in range(L_TILES):
                        round_first_half(t)
                if q == PAIRS - 1 and j == STEPS - 1:
                    start_projections(1)

            round_second_half(0)
            quantise_waiting(len(steps))
            nc.sync.dma_start(out=mixer_rows[:], in_=mixer_norm_w.partition_broadcast(P))
            nc.sync.dma_start(out=loop_rows[:], in_=loop_norm_w.partition_broadcast(P))
            early_root = keep.tile([P, 1], F32, name="early_root")
            nc.scalar.activation(out=early_root[:], in_=eps_column[:], func=ACT.Abs_reciprocal_sqrt)
        with ExitStack() as ending:
            tail = ending.enter_context(tc.tile_pool(name="tail", bufs=L_TILES))
            out_tiles = out.rearrange("b (t p) d -> (b t) p d", p=P)
            half_squares, mixed, proj_scales, residuals, res_scales, results = {}, {}, {}, {}, {}, {}

            def inverse_root(square_sum, bias, tag):
                result = tail.tile([P, 1], F32, tag=tag, name=tag)
                nc.scalar.activation(
                    out=result[:], in_=square_sum, func=ACT.Abs_reciprocal_sqrt, bias=bias,
                    scale=1.0 / D,
                )
                return result

            def square(t, half, squares):
                nc.scalar.activation(
                    out=squares[:, half * BANK : (half + 1) * BANK],
                    in_=projections[(t, half)][:], func=ACT.Square,
                    accum_out=half_squares[t][:, half : half + 1],
                )

            def mix(t, half):
                cols = slice(half * BANK, (half + 1) * BANK)
                nc.vector.tensor_tensor(
                    out=mixed[t][:, cols], in0=projections[(t, half)][:], in1=mixer_rows[:, cols],
                    op=ALU.mult,
                )

            def square_and_mix(t):
                half_squares[t] = tail.tile([P, HALVES], F32, tag="half_squares", name="half_squares")
                mixed[t] = tail.tile([P, D], F32, tag="mixed", name="mixed")
                for half in range(HALVES):
                    project_out(t, half, [OUT_PASSES - 1])
                squares = tail.tile([P, D], F32, tag="squared", name="squared")
                for half in range(HALVES):
                    if t == 0:
                        square(t, half, squares)
                        mix(t, HALVES - 1 - half)
                    else:
                        mix(t, half)
                        square(t, half, squares)
                half_mean = tail.tile([P, 1], F32, tag="half_mean")
                nc.scalar.activation(
                    out=half_mean[:], in_=half_squares[t][:, 0:1], func=ACT.Identity,
                    bias=eps_column[:, 0:1], scale=1.0 / D,
                )
                proj_scales[t] = inverse_root(
                    half_squares[t][:, 1:2], half_mean[:, 0:1], "proj_scale"
                )

            def add_residual(t):
                residuals[t] = tail.tile([P, D], F32, tag="residual", name="residual")
                nc.vector.scalar_tensor_tensor(
                    out=residuals[t][:], in0=mixed[t][:], scalar=proj_scales[t][:, 0:1],
                    in1=h_f32[:, t, :], op0=ALU.mult, op1=ALU.add,
                )
                squared = tail.tile([P, D], F32, tag="squared")
                res_squares = tail.tile([P, 1], F32, tag="res_squares")
                nc.scalar.activation(
                    out=squared[:], in_=residuals[t][:], func=ACT.Square, accum_out=res_squares[:]
                )
                res_scales[t] = inverse_root(res_squares[:], eps_column[:, 0:1], "res_scale")

            def finish(t):
                results[t] = tail.tile([P, D], F32, tag="result", name="result")
                parts = HALVES if t == L_TILES - 1 else 1
                for part in range(parts):
                    cols = slice(part * (D // parts), (part + 1) * (D // parts))
                    nc.vector.scalar_tensor_tensor(
                        out=results[t][:, cols], in0=residuals[t][:, cols],
                        scalar=res_scales[t][:, 0:1], in1=loop_rows[:, cols],
                        op0=ALU.mult, op1=ALU.mult,
                    )
                    nc.sync.dma_start(out=out_tiles[t][:, cols], in_=results[t][:, cols])

            for t in range(1, L_TILES):
                round_second_half(t)
            quantise_waiting(len(steps))
            square_and_mix(0)
            square_and_mix(1)
            start_projections(2)
            add_residual(0)
            square_and_mix(2)
            add_residual(1)
            finish(0)
            add_residual(2)
            finish(1)
            finish(2)
